import numpy as np
import ml_dtypes


def mxq(x, axis, fmt="e4m3"):
    dtype, down = {"e4m3": (ml_dtypes.float8_e4m3fn, 7), "e5m2": (ml_dtypes.float8_e5m2, 14)}[fmt]
    v = np.moveaxis(np.asarray(x, np.float32).astype(ml_dtypes.bfloat16).astype(np.float64), axis, -1)
    blocks = v.reshape(v.shape[:-1] + (-1, 32))
    amax = np.abs(blocks).max(-1, keepdims=True)
    byte = np.maximum(np.where(amax > 0, np.frexp(amax)[1] - 1 + 127, 0) - down, 1)
    scale = np.exp2(byte - 127.0)
    codes = (blocks / scale).astype(np.float32).astype(dtype).astype(np.float64)
    return np.moveaxis((codes * scale).reshape(v.shape), -1, axis)


WIDE = False


def mx_kscale(k):
    if not WIDE:
        return np.ones(k)
    levels = np.array([10, -10, 5, -5, 0])
    a = np.random.permutation(np.resize(levels, k // 512 * 4)).reshape(k // 512, 4)
    idx = np.arange(k)
    return np.exp2(a[idx // 512, idx % 128 // 32])


BF16 = ml_dtypes.bfloat16


def bf(x):
    return np.asarray(x, np.float32).astype(BF16)


def f64(x):
    return np.asarray(x).astype(np.float64)


E2M1 = np.array([0.0, 0.5, 1.0, 1.5, 2.0, 3.0, 4.0, 6.0, -0.0, -0.5, -1.0, -1.5, -2.0, -3.0, -4.0, -6.0])


def pack_weight(w, fmt):
    k, n = w.shape
    w = f64(bf(w)).reshape(k // 32, 32, n)
    amax = np.abs(w).max(1)
    if fmt == "e4m3":
        byte = np.frexp(amax)[1] - 1 + 127 - 7
    else:
        mant, ex = np.frexp(amax / 6.0)
        byte = np.where(mant > 0.5, ex, ex - 1) + 127
    byte = np.clip(np.where(amax > 0, byte, 1), 1, 254)
    scaled = (w * np.exp2(127.0 - byte)[:, None, :]).reshape(k, n).astype(np.float32)
    by_word = np.ascontiguousarray(scaled.reshape(k // 512, 128, 4, n).transpose(0, 1, 3, 2))
    if fmt == "e4m3":
        words = by_word.astype(ml_dtypes.float8_e4m3fn).view(np.uint8)
    else:
        c = by_word.astype(ml_dtypes.float4_e2m1fn).view(np.uint8) & 0xF
        words = c[..., 0::2] | (c[..., 1::2] << 4)
    return np.ascontiguousarray(words), np.ascontiguousarray(byte.astype(np.uint8).reshape(k // 512, 16, n))


def unpack_weight(words, scales, fmt):
    g, p, n, _ = words.shape
    if fmt == "e4m3":
        vals = np.ascontiguousarray(words).view(ml_dtypes.float8_e4m3fn).astype(np.float64)
    else:
        nib = np.empty((g, p, n, 4), np.uint8)
        nib[..., 0::2] = words & 0xF
        nib[..., 1::2] = words >> 4
        vals = E2M1[nib]
    vals = vals * np.repeat(np.exp2(scales.astype(np.float64) - 127.0), 8, axis=1)[..., None]
    return vals.transpose(0, 1, 3, 2).reshape(g * 512, n)


B, S, D, H, HKV, DH = 2, 4096, 1024, 2, 1, 128
HD = H * DH
KV = HKV * DH
ROPE_BASE = 10000.0
FMT = "e4m3"


def apply_rope(u):
    inv_freq = 1.0 / ROPE_BASE ** (np.arange(0, DH, 2) / DH)
    ang = np.arange(S)[:, None] * inv_freq[None, :]
    cos = np.cos(ang)[None, :, None, :]
    sin = np.sin(ang)[None, :, None, :]
    ur, ui = u[..., 0::2], u[..., 1::2]
    out = np.stack([ur * cos - ui * sin, ur * sin + ui * cos], axis=-1)
    return out.reshape(u.shape)


def setup_inputs():
    s = mx_kscale(D)
    x = bf(np.random.standard_normal((B, S, D)) * s)
    wq = np.random.standard_normal((HD, D)) / np.sqrt(D) / s[None, :]
    wk = np.random.standard_normal((KV, D)) * 1.25 / np.sqrt(D) / s[None, :]
    wv = np.random.standard_normal((KV, D)) * 1.25 / np.sqrt(D) / s[None, :]
    wq_words, wq_scales = pack_weight(np.ascontiguousarray(wq.T), FMT)
    wk_words, wk_scales = pack_weight(np.ascontiguousarray(wk.T), FMT)
    wv_words, wv_scales = pack_weight(np.ascontiguousarray(wv.T), FMT)
    return {"x": x,
            "Wq_words": wq_words, "Wq_scales": wq_scales,
            "Wk_words": wk_words, "Wk_scales": wk_scales,
            "Wv_words": wv_words, "Wv_scales": wv_scales}


def reference(x, Wq_words, Wq_scales, Wk_words, Wk_scales, Wv_words, Wv_scales):
    xq = mxq(f64(x), 2, "e4m3")
    Q = (xq @ unpack_weight(Wq_words, Wq_scales, FMT)).reshape(B, S, H, DH)
    K = (xq @ unpack_weight(Wk_words, Wk_scales, FMT)).reshape(B, S, HKV, DH)
    V = (xq @ unpack_weight(Wv_words, Wv_scales, FMT)).reshape(B, S, HKV, DH)
    Q = apply_rope(Q)
    K = apply_rope(K)
    return Q.transpose(0, 2, 1, 3), K.transpose(0, 2, 1, 3), V.transpose(0, 2, 1, 3)

@@ -1,0 +1,263 @@
+import math
+from contextlib import ExitStack
+
+import concourse.mybir as mybir
+from concourse.masks import make_identity
+
+F32 = mybir.dt.float32
+BF16 = mybir.dt.bfloat16
+I32 = mybir.dt.int32
+U32 = mybir.dt.uint32
+U8 = mybir.dt.uint8
+FP8X4 = mybir.dt.float8_e4m3fn_x4
+ALU = mybir.AluOpType
+ACT = mybir.ActivationFunctionType
+
+P = 128
+BATCH = 2
+SEQ = 4096
+D_MODEL = 1024
+HEAD = 128
+PAIRS = HEAD // 2
+DOUBLINGS = 6
+ROTATED_HEADS = 3
+N_OUT = 4 * HEAD
+K_PASS = 4 * P
+PASSES = D_MODEL // K_PASS
+PASS_WORDS = K_PASS // 2
+ROWS = SEQ // P
+RUN = 4
+SLICES = ROWS // RUN
+GROUPS = BATCH * SLICES
+X_BUFS = 6
+QUADRANTS = 4
+
+ROPE_BASE = 10000.0
+TWO_PI = 2.0 * math.pi
+ROUND_MAGIC = 1.5 * 2.0**23
+
+FLOPS = 2 * BATCH * SEQ * D_MODEL * N_OUT
+
+assert 2**DOUBLINGS == PAIRS
+
+
+def tile_multiheadattention_pa_t_kernel(
+    tc, x, wq_words, wq_scales, wk_words, wk_scales, wv_words, wv_scales, out_q, out_k, out_v
+):
+    nc = tc.nc
+    weights = (
+        (wq_words, wq_scales, 0, 2 * HEAD),
+        (wk_words, wk_scales, 2 * HEAD, HEAD),
+        (wv_words, wv_scales, 3 * HEAD, HEAD),
+    )
+    x_rows = x.rearrange("b (p r) k -> b p r k", r=ROWS)
+    q_rows = out_q.rearrange("b h (p r) d -> b p h r d", r=ROWS)
+    k_rows = out_k.rearrange("b h (p r) d -> b p h r d", r=ROWS)
+    v_rows = out_v.rearrange("b h (p r) d -> b p h r d", r=ROWS)
+
+    with ExitStack() as ctx:
+        const = ctx.enter_context(tc.tile_pool(name="const", bufs=1))
+        x_pool = ctx.enter_context(tc.tile_pool(name="x", bufs=X_BUFS))
+        quant = ctx.enter_context(tc.tile_pool(name="quant", bufs=2))
+        trig = ctx.enter_context(tc.tile_pool(name="trig", bufs=2))
+        prod_pool = ctx.enter_context(tc.tile_pool(name="products", bufs=4))
+        out_pool = ctx.enter_context(tc.tile_pool(name="results", bufs=3))
+        xt_pool = ctx.enter_context(tc.psum_pool(name="xt", bufs=3))
+        qk_pool = ctx.enter_context(tc.psum_pool(name="qk", bufs=4))
+        v_pool = ctx.enter_context(tc.psum_pool(name="v", bufs=1))
+
+        identity = const.tile([P, P], F32, name="identity")
+        make_identity(nc, identity[:])
+
+        w_codes = const.tile([P, PASSES, N_OUT], U32, name="w_codes", align_bytes=64)
+        w_planes = const.tile([P, PASSES, N_OUT], U8, name="w_planes", align_bytes=64)
+        position_int = const.tile([P, ROWS], I32, name="position_int")
+        position = const.tile([P, ROWS], F32, name="position")
+        one = const.tile([P, 1], F32, name="one")
+        turns = const.tile([P, PAIRS], F32, name="turns")
+        phase = const.tile([P, ROWS, PAIRS], F32, name="phase")
+        rounded = const.tile([P, ROWS, PAIRS], F32, name="rounded")
+        excess = const.tile([P, ROWS, PAIRS], F32, name="excess")
+        table = [
+            const.tile([P, RUN, 2, 2, PAIRS], F32, name="table%d" % c) for c in range(SLICES)
+        ]
+
+        x_tiles = {}
+        grouped = {}
+        codes = {}
+        planes = {}
+        qk_sums = {}
+        v_sums = {}
+        results = {}
+
+        def batch_and_rows(k):
+            first = RUN * (k // BATCH)
+            return k % BATCH, first, first + RUN
+
+        def load_scale_rows(scales, first, width, quadrant):
+            nc.sync.dma_start(
+                out=w_planes[32 * quadrant : 32 * quadrant + 4, :, first : first + width].bitcast(I32),
+                in_=scales[:, 4 * quadrant : 4 * quadrant + 4, :].rearrange("g r n -> r g n").bitcast(I32),
+            )
+
+        def load_x(k):
+            b, r0, r1 = batch_and_rows(k)
+            x_tiles[k] = x_pool.tile([P, RUN, D_MODEL], BF16, name="x_tile")
+            nc.sync.dma_start(out=x_tiles[k][:], in_=x_rows[b, :, r0:r1, :])
+
+        def reduce_phase(r0, r1):
+            shape = [P, r1 - r0, PAIRS]
+            nc.vector.tensor_tensor(
+                out=phase[:, r0:r1, :],
+                in0=position[:, r0:r1].unsqueeze(2).to_broadcast(shape),
+                in1=turns[:].unsqueeze(1).to_broadcast(shape),
+                op=ALU.mult,
+            )
+            nc.vector.tensor_scalar(
+                out=rounded[:, r0:r1, :], in0=phase[:, r0:r1, :], scalar1=ROUND_MAGIC, scalar2=None, op0=ALU.add
+            )
+            nc.vector.scalar_tensor_tensor(
+                out=excess[:, r0:r1, :],
+                in0=rounded[:, r0:r1, :],
+                scalar=ROUND_MAGIC,
+                in1=phase[:, r0:r1, :],
+                op0=ALU.subtract,
+                op1=ALU.subtract,
+            )
+
+        def fill_table(c):
+            away = excess[:, RUN * c : RUN * (c + 1), :]
+            nc.scalar.activation(out=table[c][:, :, 0, 1, :], in_=away, func=ACT.Sin, scale=-TWO_PI)
+            nc.scalar.activation(out=table[c][:, :, 1, 0, :], in_=away, func=ACT.Sin, scale=TWO_PI)
+            size = trig.tile([P, RUN, PAIRS], F32, name="size")
+            nc.scalar.activation(out=size[:], in_=away, func=ACT.Abs)
+            quarter = trig.tile([P, RUN, PAIRS], F32, name="quarter")
+            nc.scalar.activation(out=quarter[:], in_=size[:], func=ACT.Copy, bias=0.25, scale=-1.0)
+            for m in range(2):
+                nc.scalar.activation(out=table[c][:, :, m, m, :], in_=quarter[:], func=ACT.Sin, scale=TWO_PI)
+
+        def transpose_group(k):
+            grouped[k] = quant.tile([P, RUN, D_MODEL], BF16, name="grouped", align_bytes=64)
+            codes[k] = quant.tile([P, RUN, PASSES * P], U32, name="codes", align_bytes=64)
+            planes[k] = quant.tile([P, RUN, PASSES * P], U8, name="planes", align_bytes=64)
+            for i in range(RUN):
+                words = x_tiles[k][:, i, :].bitcast(F32)
+                flipped = xt_pool.tile([P, PASSES, 2, P], F32, name="flipped")
+                for g in range(PASSES):
+                    for u in range(2):
+                        nc.tensor.transpose(
+                            flipped[:, g, u, :],
+                            words[:, PASS_WORDS * g + u : PASS_WORDS * (g + 1) : 2],
+                            identity[:],
+                        )
+                nc.scalar.copy(
+                    out=grouped[k][:, i, :].bitcast(F32).rearrange("q (g n u) -> q g n u", g=PASSES, u=2),
+                    in_=flipped[:].rearrange("q g u n -> q g n u"),
+                )
+
+        def quantise(k, i):
+            nc.vector.quantize_mx(
+                out=codes[k][:, i, :].bitcast(FP8X4), scales=planes[k][:, i, :], in_=grouped[k][:, i, :]
+            )
+
+        def project(k):
+            results[k] = out_pool.tile([P, ROTATED_HEADS + 1, RUN, HEAD], F32, name="results")
+            v_sums[k] = v_pool.tile([P, RUN, HEAD], F32, name="v_sums")
+            for i in range(RUN):
+                qk_sums[k, i] = qk_pool.tile([P, ROTATED_HEADS, HEAD], F32, name="qk_sums")
+                qk_flat = qk_sums[k, i][:].rearrange("p h d -> p (h d)")
+                targets = (qk_flat[:, 0 : 2 * HEAD], qk_flat[:, 2 * HEAD : 3 * HEAD], v_sums[k][:, i, :])
+                for weight, target in zip(weights, targets):
+                    first, width = weight[2], weight[3]
+                    for g in range(PASSES):
+                        nc.tensor.matmul_mx(
+                            out=target,
+                            lhsT=codes[k][:, i, P * g : P * (g + 1)].bitcast(FP8X4),
+                            lhsT_scale=planes[k][:, i, P * g : P * (g + 1)],
+                            rhs=w_codes[:, g, first : first + width].bitcast(FP8X4),
+                            rhs_scale=w_planes[:, g, first : first + width],
+                            start=(g == 0),
+                            stop=(g == PASSES - 1),
+                        )
+
+        def rotate(k, i):
+            shape = [P, 2, 2, ROTATED_HEADS, PAIRS]
+            products = prod_pool.tile(shape, F32, name="products")
+            nc.vector.tensor_tensor(
+                out=products[:],
+                in0=qk_sums[k, i][:].rearrange("p h (j m) -> p m h j", m=2).unsqueeze(2).to_broadcast(shape),
+                in1=table[k // BATCH][:, i].unsqueeze(3).to_broadcast(shape),
+                op=ALU.mult,
+            )
+            nc.gpsimd.tensor_tensor(
+                out=results[k][:, 0:ROTATED_HEADS, i, :].rearrange("p h (j e) -> p h j e", e=2),
+                in0=products[:, 0].rearrange("p e h j -> p h j e"),
+                in1=products[:, 1].rearrange("p e h j -> p h j e"),
+                op=ALU.add,
+            )
+
+        def copy_values(k):
+            nc.scalar.copy(out=results[k][:, ROTATED_HEADS, :, :], in_=v_sums[k][:])
+
+        def store(k):
+            b, r0, r1 = batch_and_rows(k)
+            nc.sync.dma_start(out=q_rows[b, :, :, r0:r1, :], in_=results[k][:, 0:2, :, :])
+            nc.sync.dma_start(out=k_rows[b, :, 0, r0:r1, :], in_=results[k][:, 2, :, :])
+            nc.sync.dma_start(out=v_rows[b, :, 0, r0:r1, :], in_=results[k][:, 3, :, :])
+
+        with tc.manual_schedule():
+            nc.vector.memset(w_planes[:].bitcast(I32), 0)
+            nc.gpsimd.iota(position_int[:], pattern=[[1, ROWS]], base=0, channel_multiplier=ROWS)
+
+            scale_loads = [
+                (weight[1], weight[2], weight[3], quadrant) for weight in weights for quadrant in range(QUADRANTS)
+            ]
+            half = len(scale_loads) // 2
+            for job in scale_loads[:half]:
+                load_scale_rows(*job)
+            load_x(0)
+            load_x(1)
+            for job in scale_loads[half:]:
+                load_scale_rows(*job)
+            for k in range(2, X_BUFS - 1):
+                load_x(k)
+            for weight in weights:
+                first, width = weight[2], weight[3]
+                nc.gpsimd.dma_start(
+                    out=w_codes[:, :, first : first + width].bitcast(F32),
+                    in_=weight[0].rearrange("g p n t -> p g (n t)").bitcast(F32),
+                )
+
+            nc.vector.memset(one[:], 1.0)
+            nc.vector.tensor_scalar(out=turns[:, 0:1], in0=one[:], scalar1=1.0 / TWO_PI, scalar2=None, op0=ALU.mult)
+            for have in [2**step for step in range(DOUBLINGS)]:
+                nc.vector.tensor_scalar(
+                    out=turns[:, have : 2 * have],
+                    in0=turns[:, 0:have],
+                    scalar1=ROPE_BASE ** (-have / PAIRS),
+                    scalar2=None,
+                    op0=ALU.mult,
+                )
+            nc.vector.tensor_copy(out=position[:], in_=position_int[:])
+            reduce_phase(0, RUN)
+            fill_table(0)
+            reduce_phase(RUN, ROWS)
+
+            transpose_group(0)
+            for i in range(RUN):
+                quantise(0, i)
+
+            for k in range(GROUPS):
+                if k + X_BUFS - 1 < GROUPS:
+                    load_x(k + X_BUFS - 1)
+                if k + 1 < GROUPS:
+                    transpose_group(k + 1)
+                if k % BATCH == 0 and k // BATCH + 1 < SLICES:
+                    fill_table(k // BATCH + 1)
+                project(k)
+                for i in range(RUN):
+                    if k + 1 < GROUPS:
+                        quantise(k + 1, i)
+                    rotate(k, i)
+                copy_values(k)
+                store(k)

@@ -181,18 +181,20 @@ def tile_multiheadattention_pa_t_kernel(
                         )
 
         def rotate(k, i):
-            shape = [P, 2, 2, ROTATED_HEADS, PAIRS]
-            products = prod_pool.tile(shape, F32, name="products")
-            nc.vector.tensor_tensor(
-                out=products[:],
-                in0=qk_sums[k, i][:].rearrange("p h (j m) -> p m h j", m=2).unsqueeze(2).to_broadcast(shape),
-                in1=table[k // BATCH][:, i].unsqueeze(3).to_broadcast(shape),
-                op=ALU.mult,
-            )
+            shape = [P, ROTATED_HEADS, PAIRS, 2]
+            products = prod_pool.tile([P, 2] + shape[1:], F32, name="products")
+            members = qk_sums[k, i][:].rearrange("p h (j m) -> p m h j", m=2)
+            for m in range(2):
+                nc.vector.tensor_tensor(
+                    out=products[:, m],
+                    in0=members[:, m].unsqueeze(3).to_broadcast(shape),
+                    in1=table[k // BATCH][:, i, m].rearrange("p e j -> p j e").unsqueeze(1).to_broadcast(shape),
+                    op=ALU.mult,
+                )
             nc.gpsimd.tensor_tensor(
-                out=results[k][:, 0:ROTATED_HEADS, i, :].rearrange("p h (j e) -> p h j e", e=2),
-                in0=products[:, 0].rearrange("p e h j -> p h j e"),
-                in1=products[:, 1].rearrange("p e h j -> p h j e"),
+                out=results[k][:, 0:ROTATED_HEADS, i, :],
+                in0=products[:, 0].rearrange("p h j e -> p h (j e)"),
+                in1=products[:, 1].rearrange("p h j e -> p h (j e)"),
                 op=ALU.add,
             )
 

@@ -60,7 +60,7 @@ def tile_multiheadattention_pa_t_kernel(
         x_pool = ctx.enter_context(tc.tile_pool(name="x", bufs=X_BUFS))
         quant = ctx.enter_context(tc.tile_pool(name="quant", bufs=2))
         trig = ctx.enter_context(tc.tile_pool(name="trig", bufs=2))
-        prod_pool = ctx.enter_context(tc.tile_pool(name="products", bufs=4))
+        prod_pool = ctx.enter_context(tc.tile_pool(name="products", bufs=2))
         out_pool = ctx.enter_context(tc.tile_pool(name="results", bufs=3))
         xt_pool = ctx.enter_context(tc.psum_pool(name="xt", bufs=3))
         qk_pool = ctx.enter_context(tc.psum_pool(name="qk", bufs=4))
@@ -89,6 +89,7 @@ def tile_multiheadattention_pa_t_kernel(
         qk_sums = {}
         v_sums = {}
         results = {}
+        products = {}
 
         def batch_and_rows(k):
             first = RUN * (k // BATCH)
@@ -155,13 +156,16 @@ def tile_multiheadattention_pa_t_kernel(
                     in_=flipped[:].rearrange("q g u n -> q g n u"),
                 )
 
-        def quantise(k, i):
+        def quantise(k):
             nc.vector.quantize_mx(
-                out=codes[k][:, i, :].bitcast(FP8X4), scales=planes[k][:, i, :], in_=grouped[k][:, i, :]
+                out=codes[k][:].rearrange("q i n -> q (i n)").bitcast(FP8X4),
+                scales=planes[k][:].rearrange("q i n -> q (i n)"),
+                in_=grouped[k][:].rearrange("q i n -> q (i n)"),
             )
 
         def project(k):
             results[k] = out_pool.tile([P, ROTATED_HEADS + 1, RUN, HEAD], F32, name="results")
+            products[k] = prod_pool.tile([P, RUN, 2, ROTATED_HEADS, PAIRS, 2], F32, name="products")
             v_sums[k] = v_pool.tile([P, RUN, HEAD], F32, name="v_sums")
             for i in range(RUN):
                 qk_sums[k, i] = qk_pool.tile([P, ROTATED_HEADS, HEAD], F32, name="qk_sums")
@@ -180,21 +184,22 @@ def tile_multiheadattention_pa_t_kernel(
                             stop=(g == PASSES - 1),
                         )
 
-        def rotate(k, i):
+        def multiply(k, i):
             shape = [P, ROTATED_HEADS, PAIRS, 2]
-            products = prod_pool.tile([P, 2] + shape[1:], F32, name="products")
             members = qk_sums[k, i][:].rearrange("p h (j m) -> p m h j", m=2)
             for m in range(2):
                 nc.vector.tensor_tensor(
-                    out=products[:, m],
+                    out=products[k][:, i, m],
                     in0=members[:, m].unsqueeze(3).to_broadcast(shape),
                     in1=table[k // BATCH][:, i, m].rearrange("p e j -> p j e").unsqueeze(1).to_broadcast(shape),
                     op=ALU.mult,
                 )
+
+        def add(k):
             nc.gpsimd.tensor_tensor(
-                out=results[k][:, 0:ROTATED_HEADS, i, :],
-                in0=products[:, 0].rearrange("p h j e -> p h (j e)"),
-                in1=products[:, 1].rearrange("p h j e -> p h (j e)"),
+                out=results[k][:, 0:ROTATED_HEADS, :, :].rearrange("p h i d -> p i h d"),
+                in0=products[k][:, :, 0].rearrange("p i h j e -> p i h (j e)"),
+                in1=products[k][:, :, 1].rearrange("p i h j e -> p i h (j e)"),
                 op=ALU.add,
             )
 
@@ -246,8 +251,7 @@ def tile_multiheadattention_pa_t_kernel(
             reduce_phase(RUN, ROWS)
 
             transpose_group(0)
-            for i in range(RUN):
-                quantise(0, i)
+            quantise(0)
 
             for k in range(GROUPS):
                 if k + X_BUFS - 1 < GROUPS:
@@ -257,9 +261,10 @@ def tile_multiheadattention_pa_t_kernel(
                 if k % BATCH == 0 and k // BATCH + 1 < SLICES:
                     fill_table(k // BATCH + 1)
                 project(k)
+                if k + 1 < GROUPS:
+                    quantise(k + 1)
                 for i in range(RUN):
-                    if k + 1 < GROUPS:
-                        quantise(k + 1, i)
-                    rotate(k, i)
+                    multiply(k, i)
+                add(k)
                 copy_values(k)
                 store(k)

@@ -30,6 +30,7 @@ RUN = 4
 SLICES = ROWS // RUN
 GROUPS = BATCH * SLICES
 X_BUFS = 6
+LOOKAHEAD = 2
 QUADRANTS = 4
 
 ROPE_BASE = 10000.0
@@ -59,6 +60,7 @@ def tile_multiheadattention_pa_t_kernel(
         const = ctx.enter_context(tc.tile_pool(name="const", bufs=1))
         x_pool = ctx.enter_context(tc.tile_pool(name="x", bufs=X_BUFS))
         quant = ctx.enter_context(tc.tile_pool(name="quant", bufs=2))
+        code_pool = ctx.enter_context(tc.tile_pool(name="codes", bufs=LOOKAHEAD + 1))
         trig = ctx.enter_context(tc.tile_pool(name="trig", bufs=2))
         prod_pool = ctx.enter_context(tc.tile_pool(name="products", bufs=2))
         out_pool = ctx.enter_context(tc.tile_pool(name="results", bufs=3))
@@ -139,8 +141,8 @@ def tile_multiheadattention_pa_t_kernel(
 
         def transpose_group(k):
             grouped[k] = quant.tile([P, RUN, D_MODEL], BF16, name="grouped", align_bytes=64)
-            codes[k] = quant.tile([P, RUN, PASSES * P], U32, name="codes", align_bytes=64)
-            planes[k] = quant.tile([P, RUN, PASSES * P], U8, name="planes", align_bytes=64)
+            codes[k] = code_pool.tile([P, RUN, PASSES * P], U32, name="codes", align_bytes=64)
+            planes[k] = code_pool.tile([P, RUN, PASSES * P], U8, name="planes", align_bytes=64)
             for i in range(RUN):
                 words = x_tiles[k][:, i, :].bitcast(F32)
                 flipped = xt_pool.tile([P, PASSES, 2, P], F32, name="flipped")
@@ -250,21 +252,23 @@ def tile_multiheadattention_pa_t_kernel(
             fill_table(0)
             reduce_phase(RUN, ROWS)
 
-            transpose_group(0)
-            quantise(0)
+            for k in range(LOOKAHEAD):
+                transpose_group(k)
+            for k in range(LOOKAHEAD):
+                quantise(k)
 
             for k in range(GROUPS):
                 if k + X_BUFS - 1 < GROUPS:
                     load_x(k + X_BUFS - 1)
-                if k + 1 < GROUPS:
-                    transpose_group(k + 1)
+                if k + LOOKAHEAD < GROUPS:
+                    transpose_group(k + LOOKAHEAD)
                 if k % BATCH == 0 and k // BATCH + 1 < SLICES:
                     fill_table(k // BATCH + 1)
                 project(k)
-                if k + 1 < GROUPS:
-                    quantise(k + 1)
                 for i in range(RUN):
                     multiply(k, i)
                 add(k)
+                if k + LOOKAHEAD < GROUPS:
+                    quantise(k + LOOKAHEAD)
                 copy_values(k)
                 store(k)

@@ -64,9 +64,8 @@ def tile_multiheadattention_pa_t_kernel(
         trig = ctx.enter_context(tc.tile_pool(name="trig", bufs=2))
         prod_pool = ctx.enter_context(tc.tile_pool(name="products", bufs=2))
         out_pool = ctx.enter_context(tc.tile_pool(name="results", bufs=3))
-        xt_pool = ctx.enter_context(tc.psum_pool(name="xt", bufs=3))
-        qk_pool = ctx.enter_context(tc.psum_pool(name="qk", bufs=4))
-        v_pool = ctx.enter_context(tc.psum_pool(name="v", bufs=1))
+        xt_pool = ctx.enter_context(tc.psum_pool(name="xt", bufs=4))
+        sum_pool = ctx.enter_context(tc.psum_pool(name="sums", bufs=4))
 
         identity = const.tile([P, P], F32, name="identity")
         make_identity(nc, identity[:])
@@ -88,8 +87,7 @@ def tile_multiheadattention_pa_t_kernel(
         grouped = {}
         codes = {}
         planes = {}
-        qk_sums = {}
-        v_sums = {}
+        sums = {}
         results = {}
         products = {}
 
@@ -168,27 +166,22 @@ def tile_multiheadattention_pa_t_kernel(
         def project(k):
             results[k] = out_pool.tile([P, ROTATED_HEADS + 1, RUN, HEAD], F32, name="results")
             products[k] = prod_pool.tile([P, RUN, 2, ROTATED_HEADS, PAIRS, 2], F32, name="products")
-            v_sums[k] = v_pool.tile([P, RUN, HEAD], F32, name="v_sums")
             for i in range(RUN):
-                qk_sums[k, i] = qk_pool.tile([P, ROTATED_HEADS, HEAD], F32, name="qk_sums")
-                qk_flat = qk_sums[k, i][:].rearrange("p h d -> p (h d)")
-                targets = (qk_flat[:, 0 : 2 * HEAD], qk_flat[:, 2 * HEAD : 3 * HEAD], v_sums[k][:, i, :])
-                for weight, target in zip(weights, targets):
-                    first, width = weight[2], weight[3]
-                    for g in range(PASSES):
-                        nc.tensor.matmul_mx(
-                            out=target,
-                            lhsT=codes[k][:, i, P * g : P * (g + 1)].bitcast(FP8X4),
-                            lhsT_scale=planes[k][:, i, P * g : P * (g + 1)],
-                            rhs=w_codes[:, g, first : first + width].bitcast(FP8X4),
-                            rhs_scale=w_planes[:, g, first : first + width],
-                            start=(g == 0),
-                            stop=(g == PASSES - 1),
-                        )
+                sums[k, i] = sum_pool.tile([P, ROTATED_HEADS + 1, HEAD], F32, name="sums")
+                for g in range(PASSES):
+                    nc.tensor.matmul_mx(
+                        out=sums[k, i][:].rearrange("p h d -> p (h d)"),
+                        lhsT=codes[k][:, i, P * g : P * (g + 1)].bitcast(FP8X4),
+                        lhsT_scale=planes[k][:, i, P * g : P * (g + 1)],
+                        rhs=w_codes[:, g, :].bitcast(FP8X4),
+                        rhs_scale=w_planes[:, g, :],
+                        start=(g == 0),
+                        stop=(g == PASSES - 1),
+                    )
 
         def multiply(k, i):
             shape = [P, ROTATED_HEADS, PAIRS, 2]
-            members = qk_sums[k, i][:].rearrange("p h (j m) -> p m h j", m=2)
+            members = sums[k, i][:, 0:ROTATED_HEADS, :].rearrange("p h (j m) -> p m h j", m=2)
             for m in range(2):
                 nc.vector.tensor_tensor(
                     out=products[k][:, i, m],
@@ -205,8 +198,8 @@ def tile_multiheadattention_pa_t_kernel(
                 op=ALU.add,
             )
 
-        def copy_values(k):
-            nc.scalar.copy(out=results[k][:, ROTATED_HEADS, :, :], in_=v_sums[k][:])
+        def copy_values(k, i):
+            nc.scalar.copy(out=results[k][:, ROTATED_HEADS, i, :], in_=sums[k, i][:, ROTATED_HEADS, :])
 
         def store(k):
             b, r0, r1 = batch_and_rows(k)
@@ -266,9 +259,10 @@ def tile_multiheadattention_pa_t_kernel(
                     fill_table(k // BATCH + 1)
                 project(k)
                 for i in range(RUN):
+                    copy_values(k, i)
+                for i in range(RUN):
                     multiply(k, i)
                 add(k)
                 if k + LOOKAHEAD < GROUPS:
                     quantise(k + LOOKAHEAD)
-                copy_values(k)
                 store(k)

@@ -78,9 +78,9 @@ def tile_multiheadattention_pa_t_kernel(
         turns = const.tile([P, PAIRS], F32, name="turns")
         phase = const.tile([P, ROWS, PAIRS], F32, name="phase")
         rounded = const.tile([P, ROWS, PAIRS], F32, name="rounded")
-        excess = const.tile([P, ROWS, PAIRS], F32, name="excess")
+        excess = const.tile([P, 2, ROWS, PAIRS], F32, name="excess")
         table = [
-            const.tile([P, RUN, 2, 2, PAIRS], F32, name="table%d" % c) for c in range(SLICES)
+            const.tile([P, RUN, 2, PAIRS, 2], F32, name="table%d" % c) for c in range(SLICES)
         ]
 
         x_tiles = {}
@@ -118,7 +118,7 @@ def tile_multiheadattention_pa_t_kernel(
                 out=rounded[:, r0:r1, :], in0=phase[:, r0:r1, :], scalar1=ROUND_MAGIC, scalar2=None, op0=ALU.add
             )
             nc.vector.scalar_tensor_tensor(
-                out=excess[:, r0:r1, :],
+                out=excess[:, 1, r0:r1, :],
                 in0=rounded[:, r0:r1, :],
                 scalar=ROUND_MAGIC,
                 in1=phase[:, r0:r1, :],
@@ -127,15 +127,24 @@ def tile_multiheadattention_pa_t_kernel(
             )
 
         def fill_table(c):
-            away = excess[:, RUN * c : RUN * (c + 1), :]
-            nc.scalar.activation(out=table[c][:, :, 0, 1, :], in_=away, func=ACT.Sin, scale=-TWO_PI)
-            nc.scalar.activation(out=table[c][:, :, 1, 0, :], in_=away, func=ACT.Sin, scale=TWO_PI)
+            rows = slice(RUN * c, RUN * (c + 1))
+            shape = [P, RUN, PAIRS, 2]
             size = trig.tile([P, RUN, PAIRS], F32, name="size")
-            nc.scalar.activation(out=size[:], in_=away, func=ACT.Abs)
-            quarter = trig.tile([P, RUN, PAIRS], F32, name="quarter")
-            nc.scalar.activation(out=quarter[:], in_=size[:], func=ACT.Copy, bias=0.25, scale=-1.0)
-            for m in range(2):
-                nc.scalar.activation(out=table[c][:, :, m, m, :], in_=quarter[:], func=ACT.Sin, scale=TWO_PI)
+            nc.scalar.activation(out=size[:], in_=excess[:, 1, rows, :], func=ACT.Abs)
+            nc.scalar.activation(out=excess[:, 0, rows, :], in_=excess[:, 1, rows, :], func=ACT.Copy, scale=-1.0)
+            nc.scalar.activation(
+                out=table[c][:, :, 0, :, :],
+                in_=size[:].unsqueeze(3).to_broadcast(shape),
+                func=ACT.Sin,
+                scale=-TWO_PI,
+                bias=0.25 * TWO_PI,
+            )
+            nc.scalar.activation(
+                out=table[c][:, :, 1, :, :],
+                in_=excess[:, :, rows, :].rearrange("p m r j -> p r j m"),
+                func=ACT.Sin,
+                scale=TWO_PI,
+            )
 
         def transpose_group(k):
             grouped[k] = quant.tile([P, RUN, D_MODEL], BF16, name="grouped", align_bytes=64)
@@ -165,7 +174,7 @@ def tile_multiheadattention_pa_t_kernel(
 
         def project(k):
             results[k] = out_pool.tile([P, ROTATED_HEADS + 1, RUN, HEAD], F32, name="results")
-            products[k] = prod_pool.tile([P, RUN, 2, ROTATED_HEADS, PAIRS, 2], F32, name="products")
+            products[k] = prod_pool.tile([P, RUN, 2, ROTATED_HEADS, HEAD], F32, name="products")
             for i in range(RUN):
                 sums[k, i] = sum_pool.tile([P, ROTATED_HEADS + 1, HEAD], F32, name="sums")
                 for g in range(PASSES):
@@ -180,21 +189,21 @@ def tile_multiheadattention_pa_t_kernel(
                     )
 
         def multiply(k, i):
-            shape = [P, ROTATED_HEADS, PAIRS, 2]
-            members = sums[k, i][:, 0:ROTATED_HEADS, :].rearrange("p h (j m) -> p m h j", m=2)
-            for m in range(2):
-                nc.vector.tensor_tensor(
-                    out=products[k][:, i, m],
-                    in0=members[:, m].unsqueeze(3).to_broadcast(shape),
-                    in1=table[k // BATCH][:, i, m].rearrange("p e j -> p j e").unsqueeze(1).to_broadcast(shape),
-                    op=ALU.mult,
-                )
+            shape = [P, 2, ROTATED_HEADS, HEAD]
+            nc.vector.tensor_tensor(
+                out=products[k][:, i],
+                in0=sums[k, i][:, 0:ROTATED_HEADS, :].unsqueeze(1).to_broadcast(shape),
+                in1=table[k // BATCH][:, i].rearrange("p a j m -> p a (j m)").unsqueeze(2).to_broadcast(shape),
+                op=ALU.mult,
+            )
 
         def add(k):
+            own = products[k][:, :, 0].rearrange("p i h (j m) -> p i h j m", m=2)
+            other = products[k][:, :, 1].rearrange("p i h (j m) -> p i h j m", m=2)
             nc.gpsimd.tensor_tensor(
-                out=results[k][:, 0:ROTATED_HEADS, :, :].rearrange("p h i d -> p i h d"),
-                in0=products[k][:, :, 0].rearrange("p i h j e -> p i h (j e)"),
-                in1=products[k][:, :, 1].rearrange("p i h j e -> p i h (j e)"),
+                out=results[k][:, 0:ROTATED_HEADS, :, :].rearrange("p h i (j e) -> p i h j e", e=2),
+                in0=own,
+                in1=other[:, :, :, :, ::-1],
                 op=ALU.add,
             )
 

@@ -63,7 +63,7 @@ def tile_multiheadattention_pa_t_kernel(
         code_pool = ctx.enter_context(tc.tile_pool(name="codes", bufs=LOOKAHEAD + 1))
         trig = ctx.enter_context(tc.tile_pool(name="trig", bufs=2))
         prod_pool = ctx.enter_context(tc.tile_pool(name="products", bufs=2))
-        out_pool = ctx.enter_context(tc.tile_pool(name="results", bufs=3))
+        out_pool = ctx.enter_context(tc.tile_pool(name="results", bufs=6))
         xt_pool = ctx.enter_context(tc.psum_pool(name="xt", bufs=4))
         sum_pool = ctx.enter_context(tc.psum_pool(name="sums", bufs=4))
 
@@ -90,6 +90,9 @@ def tile_multiheadattention_pa_t_kernel(
         sums = {}
         results = {}
         products = {}
+
+        def pieces(k):
+            return 2 if k >= GROUPS - 2 else 1
 
         def batch_and_rows(k):
             first = RUN * (k // BATCH)
@@ -173,7 +176,10 @@ def tile_multiheadattention_pa_t_kernel(
             )
 
         def project(k):
-            results[k] = out_pool.tile([P, ROTATED_HEADS + 1, RUN, HEAD], F32, name="results")
+            span = RUN // pieces(k)
+            results[k] = [
+                out_pool.tile([P, ROTATED_HEADS + 1, span, HEAD], F32, name="results") for piece in range(pieces(k))
+            ]
             products[k] = prod_pool.tile([P, RUN, 2, ROTATED_HEADS, HEAD], F32, name="products")
             for i in range(RUN):
                 sums[k, i] = sum_pool.tile([P, ROTATED_HEADS + 1, HEAD], F32, name="sums")
@@ -197,24 +203,30 @@ def tile_multiheadattention_pa_t_kernel(
                 op=ALU.mult,
             )
 
-        def add(k):
-            own = products[k][:, :, 0].rearrange("p i h (j m) -> p i h j m", m=2)
-            other = products[k][:, :, 1].rearrange("p i h (j m) -> p i h j m", m=2)
-            nc.gpsimd.tensor_tensor(
-                out=results[k][:, 0:ROTATED_HEADS, :, :].rearrange("p h i (j e) -> p i h j e", e=2),
+        def add(engine, k, piece):
+            span = RUN // pieces(k)
+            tiles = slice(span * piece, span * (piece + 1))
+            own = products[k][:, tiles, 0].rearrange("p i h (j m) -> p i h j m", m=2)
+            other = products[k][:, tiles, 1].rearrange("p i h (j m) -> p i h j m", m=2)
+            engine.tensor_tensor(
+                out=results[k][piece][:, 0:ROTATED_HEADS, :, :].rearrange("p h i (j e) -> p i h j e", e=2),
                 in0=own,
                 in1=other[:, :, :, :, ::-1],
                 op=ALU.add,
             )
 
         def copy_values(k, i):
-            nc.scalar.copy(out=results[k][:, ROTATED_HEADS, i, :], in_=sums[k, i][:, ROTATED_HEADS, :])
+            piece, local = divmod(i, RUN // pieces(k))
+            nc.scalar.copy(out=results[k][piece][:, ROTATED_HEADS, local, :], in_=sums[k, i][:, ROTATED_HEADS, :])
 
-        def store(k):
-            b, r0, r1 = batch_and_rows(k)
-            nc.sync.dma_start(out=q_rows[b, :, :, r0:r1, :], in_=results[k][:, 0:2, :, :])
-            nc.sync.dma_start(out=k_rows[b, :, 0, r0:r1, :], in_=results[k][:, 2, :, :])
-            nc.sync.dma_start(out=v_rows[b, :, 0, r0:r1, :], in_=results[k][:, 3, :, :])
+        def store(k, piece):
+            b, first, beyond = batch_and_rows(k)
+            span = RUN // pieces(k)
+            r0 = first + span * piece
+            r1 = r0 + span
+            nc.sync.dma_start(out=q_rows[b, :, :, r0:r1, :], in_=results[k][piece][:, 0:2, :, :])
+            nc.sync.dma_start(out=k_rows[b, :, 0, r0:r1, :], in_=results[k][piece][:, 2, :, :])
+            nc.sync.dma_start(out=v_rows[b, :, 0, r0:r1, :], in_=results[k][piece][:, 3, :, :])
 
         with tc.manual_schedule():
             nc.vector.memset(w_planes[:].bitcast(I32), 0)
@@ -271,7 +283,11 @@ def tile_multiheadattention_pa_t_kernel(
                     copy_values(k, i)
                 for i in range(RUN):
                     multiply(k, i)
-                add(k)
+                adder = nc.gpsimd if k < GROUPS - 1 else nc.vector
+                add(adder, k, 0)
                 if k + LOOKAHEAD < GROUPS:
                     quantise(k + LOOKAHEAD)
-                store(k)
+                store(k, 0)
+                for piece in range(1, pieces(k)):
+                    add(adder, k, piece)
+                    store(k, piece)

@@ -242,7 +242,7 @@ def tile_multiheadattention_pa_t_kernel(
             load_x(1)
             for job in scale_loads[half:]:
                 load_scale_rows(*job)
-            for k in range(2, X_BUFS - 1):
+            for k in range(2, X_BUFS):
                 load_x(k)
             for weight in weights:
                 first, width = weight[2], weight[3]
@@ -268,14 +268,15 @@ def tile_multiheadattention_pa_t_kernel(
 
             for k in range(LOOKAHEAD):
                 transpose_group(k)
+                load_x(k + X_BUFS)
             for k in range(LOOKAHEAD):
                 quantise(k)
 
             for k in range(GROUPS):
-                if k + X_BUFS - 1 < GROUPS:
-                    load_x(k + X_BUFS - 1)
                 if k + LOOKAHEAD < GROUPS:
                     transpose_group(k + LOOKAHEAD)
+                if k + LOOKAHEAD + X_BUFS < GROUPS:
+                    load_x(k + LOOKAHEAD + X_BUFS)
                 if k % BATCH == 0 and k // BATCH + 1 < SLICES:
                     fill_table(k // BATCH + 1)
                 project(k)

@@ -19,7 +19,6 @@ SEQ = 4096
 D_MODEL = 1024
 HEAD = 128
 PAIRS = HEAD // 2
-DOUBLINGS = 6
 ROTATED_HEADS = 3
 N_OUT = 4 * HEAD
 K_PASS = 4 * P
@@ -30,6 +29,7 @@ RUN = 4
 SLICES = ROWS // RUN
 GROUPS = BATCH * SLICES
 X_BUFS = 6
+TABLE_PARTS = 6
 LOOKAHEAD = 2
 QUADRANTS = 4
 
@@ -39,7 +39,8 @@ ROUND_MAGIC = 1.5 * 2.0**23
 
 FLOPS = 2 * BATCH * SEQ * D_MODEL * N_OUT
 
-assert 2**DOUBLINGS == PAIRS
+assert 4**3 == PAIRS
+assert TABLE_PARTS == BATCH * (RUN - 1)
 
 
 def tile_multiheadattention_pa_t_kernel(
@@ -89,6 +90,7 @@ def tile_multiheadattention_pa_t_kernel(
         planes = {}
         sums = {}
         results = {}
+        sizes = {}
         products = {}
 
         def pieces(k):
@@ -109,45 +111,55 @@ def tile_multiheadattention_pa_t_kernel(
             x_tiles[k] = x_pool.tile([P, RUN, D_MODEL], BF16, name="x_tile")
             nc.sync.dma_start(out=x_tiles[k][:], in_=x_rows[b, :, r0:r1, :])
 
-        def reduce_phase(r0, r1):
-            shape = [P, r1 - r0, PAIRS]
-            nc.vector.tensor_tensor(
-                out=phase[:, r0:r1, :],
-                in0=position[:, r0:r1].unsqueeze(2).to_broadcast(shape),
-                in1=turns[:].unsqueeze(1).to_broadcast(shape),
-                op=ALU.mult,
-            )
-            nc.vector.tensor_scalar(
-                out=rounded[:, r0:r1, :], in0=phase[:, r0:r1, :], scalar1=ROUND_MAGIC, scalar2=None, op0=ALU.add
-            )
-            nc.vector.scalar_tensor_tensor(
-                out=excess[:, 1, r0:r1, :],
-                in0=rounded[:, r0:r1, :],
-                scalar=ROUND_MAGIC,
-                in1=phase[:, r0:r1, :],
-                op0=ALU.subtract,
-                op1=ALU.subtract,
-            )
+        def reduce_phase(*chunks):
+            for r0, r1 in chunks:
+                shape = [P, r1 - r0, PAIRS]
+                nc.vector.tensor_tensor(
+                    out=phase[:, r0:r1, :],
+                    in0=position[:, r0:r1].unsqueeze(2).to_broadcast(shape),
+                    in1=turns[:].unsqueeze(1).to_broadcast(shape),
+                    op=ALU.mult,
+                )
+            for r0, r1 in chunks:
+                nc.vector.tensor_scalar(
+                    out=rounded[:, r0:r1, :], in0=phase[:, r0:r1, :], scalar1=ROUND_MAGIC, scalar2=None, op0=ALU.add
+                )
+            for r0, r1 in chunks:
+                nc.vector.scalar_tensor_tensor(
+                    out=excess[:, 1, r0:r1, :],
+                    in0=rounded[:, r0:r1, :],
+                    scalar=ROUND_MAGIC,
+                    in1=phase[:, r0:r1, :],
+                    op0=ALU.subtract,
+                    op1=ALU.subtract,
+                )
 
-        def fill_table(c):
+        def fill_table(c, part):
             rows = slice(RUN * c, RUN * (c + 1))
-            shape = [P, RUN, PAIRS, 2]
-            size = trig.tile([P, RUN, PAIRS], F32, name="size")
-            nc.scalar.activation(out=size[:], in_=excess[:, 1, rows, :], func=ACT.Abs)
-            nc.scalar.activation(out=excess[:, 0, rows, :], in_=excess[:, 1, rows, :], func=ACT.Copy, scale=-1.0)
-            nc.scalar.activation(
-                out=table[c][:, :, 0, :, :],
-                in_=size[:].unsqueeze(3).to_broadcast(shape),
-                func=ACT.Sin,
-                scale=-TWO_PI,
-                bias=0.25 * TWO_PI,
-            )
-            nc.scalar.activation(
-                out=table[c][:, :, 1, :, :],
-                in_=excess[:, :, rows, :].rearrange("p m r j -> p r j m"),
-                func=ACT.Sin,
-                scale=TWO_PI,
-            )
+            if part == 0:
+                sizes[c] = trig.tile([P, RUN, PAIRS], F32, name="size")
+                nc.scalar.activation(out=sizes[c][:], in_=excess[:, 1, rows, :], func=ACT.Abs)
+            elif part == 1:
+                nc.scalar.activation(out=excess[:, 0, rows, :], in_=excess[:, 1, rows, :], func=ACT.Copy, scale=-1.0)
+            else:
+                a, half = divmod(part - 2, 2)
+                i0 = half * (RUN // 2)
+                i1 = i0 + RUN // 2
+                if a == 0:
+                    nc.scalar.activation(
+                        out=table[c][:, i0:i1, 0, :, :],
+                        in_=sizes[c][:, i0:i1, :].unsqueeze(3).to_broadcast([P, RUN // 2, PAIRS, 2]),
+                        func=ACT.Sin,
+                        scale=-TWO_PI,
+                        bias=0.25 * TWO_PI,
+                    )
+                else:
+                    nc.scalar.activation(
+                        out=table[c][:, i0:i1, 1, :, :],
+                        in_=excess[:, :, RUN * c + i0 : RUN * c + i1, :].rearrange("p m r j -> p r j m"),
+                        func=ACT.Sin,
+                        scale=TWO_PI,
+                    )
 
         def transpose_group(k):
             grouped[k] = quant.tile([P, RUN, D_MODEL], BF16, name="grouped", align_bytes=64)
@@ -236,9 +248,9 @@ def tile_multiheadattention_pa_t_kernel(
                 (weight[1], weight[2], weight[3], quadrant) for weight in weights for quadrant in range(QUADRANTS)
             ]
             half = len(scale_loads) // 2
+            load_x(0)
             for job in scale_loads[:half]:
                 load_scale_rows(*job)
-            load_x(0)
             load_x(1)
             for job in scale_loads[half:]:
                 load_scale_rows(*job)
@@ -246,25 +258,27 @@ def tile_multiheadattention_pa_t_kernel(
                 load_x(k)
             for weight in weights:
                 first, width = weight[2], weight[3]
-                nc.gpsimd.dma_start(
+                nc.scalar.dma_start(
                     out=w_codes[:, :, first : first + width].bitcast(F32),
                     in_=weight[0].rearrange("g p n t -> p g (n t)").bitcast(F32),
                 )
 
             nc.vector.memset(one[:], 1.0)
             nc.vector.tensor_scalar(out=turns[:, 0:1], in0=one[:], scalar1=1.0 / TWO_PI, scalar2=None, op0=ALU.mult)
-            for have in [2**step for step in range(DOUBLINGS)]:
-                nc.vector.tensor_scalar(
-                    out=turns[:, have : 2 * have],
-                    in0=turns[:, 0:have],
-                    scalar1=ROPE_BASE ** (-have / PAIRS),
-                    scalar2=None,
-                    op0=ALU.mult,
-                )
+            for have in (1, 4, 16):
+                for m in range(1, 4):
+                    nc.vector.tensor_scalar(
+                        out=turns[:, m * have : (m + 1) * have],
+                        in0=turns[:, 0:have],
+                        scalar1=ROPE_BASE ** (-m * have / PAIRS),
+                        scalar2=None,
+                        op0=ALU.mult,
+                    )
             nc.vector.tensor_copy(out=position[:], in_=position_int[:])
-            reduce_phase(0, RUN)
-            fill_table(0)
-            reduce_phase(RUN, ROWS)
+            reduce_phase((0, RUN), (RUN, ROWS // 2))
+            for part in range(TABLE_PARTS):
+                fill_table(0, part)
+            reduce_phase((ROWS // 2, 3 * ROWS // 4), (3 * ROWS // 4, ROWS))
 
             for k in range(LOOKAHEAD):
                 transpose_group(k)
@@ -277,11 +291,11 @@ def tile_multiheadattention_pa_t_kernel(
                     transpose_group(k + LOOKAHEAD)
                 if k + LOOKAHEAD + X_BUFS < GROUPS:
                     load_x(k + LOOKAHEAD + X_BUFS)
-                if k % BATCH == 0 and k // BATCH + 1 < SLICES:
-                    fill_table(k // BATCH + 1)
                 project(k)
                 for i in range(RUN):
                     copy_values(k, i)
+                    if i > 0 and k // BATCH + 1 < SLICES:
+                        fill_table(k // BATCH + 1, (RUN - 1) * (k % BATCH) + i - 1)
                 for i in range(RUN):
                     multiply(k, i)
                 adder = nc.gpsimd if k < GROUPS - 1 else nc.vector

@@ -76,6 +76,7 @@ def tile_multiheadattention_pa_t_kernel(
         position_int = const.tile([P, ROWS], I32, name="position_int")
         position = const.tile([P, ROWS], F32, name="position")
         one = const.tile([P, 1], F32, name="one")
+        warm = const.tile([P, 2], F32, name="warm")
         turns = const.tile([P, PAIRS], F32, name="turns")
         phase = const.tile([P, ROWS, PAIRS], F32, name="phase")
         rounded = const.tile([P, ROWS, PAIRS], F32, name="rounded")
@@ -242,26 +243,29 @@ def tile_multiheadattention_pa_t_kernel(
 
         with tc.manual_schedule():
             nc.vector.memset(w_planes[:].bitcast(I32), 0)
+            nc.gpsimd.memset(warm[:, 0:1], 0.0)
+            nc.scalar.activation(out=warm[:, 1:2], in_=warm[:, 0:1], func=ACT.Sin)
             nc.gpsimd.iota(position_int[:], pattern=[[1, ROWS]], base=0, channel_multiplier=ROWS)
 
             scale_loads = [
                 (weight[1], weight[2], weight[3], quadrant) for weight in weights for quadrant in range(QUADRANTS)
             ]
-            half = len(scale_loads) // 2
             load_x(0)
-            for job in scale_loads[:half]:
+            for job in scale_loads[0:6]:
                 load_scale_rows(*job)
             load_x(1)
-            for job in scale_loads[half:]:
-                load_scale_rows(*job)
-            for k in range(2, X_BUFS):
-                load_x(k)
+            load_scale_rows(*scale_loads[6])
             for weight in weights:
                 first, width = weight[2], weight[3]
                 nc.scalar.dma_start(
                     out=w_codes[:, :, first : first + width].bitcast(F32),
                     in_=weight[0].rearrange("g p n t -> p g (n t)").bitcast(F32),
                 )
+            load_x(2)
+            for job in scale_loads[7:]:
+                load_scale_rows(*job)
+            for k in range(3, X_BUFS):
+                load_x(k)
 
             nc.vector.memset(one[:], 1.0)
             nc.vector.tensor_scalar(out=turns[:, 0:1], in0=one[:], scalar1=1.0 / TWO_PI, scalar2=None, op0=ALU.mult)

@@ -30,6 +30,8 @@ SLICES = ROWS // RUN
 GROUPS = BATCH * SLICES
 X_BUFS = 6
 TABLE_PARTS = 6
+WARM_FIRST = 7
+WARM_BETWEEN = 2
 LOOKAHEAD = 2
 QUADRANTS = 4
 
@@ -76,6 +78,7 @@ def tile_multiheadattention_pa_t_kernel(
         position_int = const.tile([P, ROWS], I32, name="position_int")
         position = const.tile([P, ROWS], F32, name="position")
         one = const.tile([P, 1], F32, name="one")
+        idle_work = const.tile([P, N_OUT], BF16, name="idle_work")
         warm = const.tile([P, 2], F32, name="warm")
         turns = const.tile([P, PAIRS], F32, name="turns")
         phase = const.tile([P, ROWS, PAIRS], F32, name="phase")
@@ -188,6 +191,17 @@ def tile_multiheadattention_pa_t_kernel(
                 in_=grouped[k][:].rearrange("q i n -> q (i n)"),
             )
 
+        def keep_warm(count):
+            unread = sum_pool.tile([P, ROTATED_HEADS + 1, HEAD], F32, name="sums")
+            for n in range(count):
+                nc.tensor.matmul(
+                    out=unread[:].rearrange("p h d -> p (h d)"),
+                    lhsT=idle_work[:, 0:P],
+                    rhs=idle_work[:],
+                    start=True,
+                    stop=True,
+                )
+
         def project(k):
             span = RUN // pieces(k)
             results[k] = [
@@ -243,6 +257,7 @@ def tile_multiheadattention_pa_t_kernel(
 
         with tc.manual_schedule():
             nc.vector.memset(w_planes[:].bitcast(I32), 0)
+            nc.gpsimd.memset(idle_work[:], 0.0)
             nc.gpsimd.memset(warm[:, 0:1], 0.0)
             nc.scalar.activation(out=warm[:, 1:2], in_=warm[:, 0:1], func=ACT.Sin)
             nc.gpsimd.iota(position_int[:], pattern=[[1, ROWS]], base=0, channel_multiplier=ROWS)
@@ -284,9 +299,11 @@ def tile_multiheadattention_pa_t_kernel(
                 fill_table(0, part)
             reduce_phase((ROWS // 2, 3 * ROWS // 4), (3 * ROWS // 4, ROWS))
 
+            keep_warm(WARM_FIRST)
             for k in range(LOOKAHEAD):
                 transpose_group(k)
                 load_x(k + X_BUFS)
+                keep_warm(WARM_BETWEEN)
             for k in range(LOOKAHEAD):
                 quantise(k)
 
@@ -295,6 +312,8 @@ def tile_multiheadattention_pa_t_kernel(
                     transpose_group(k + LOOKAHEAD)
                 if k + LOOKAHEAD + X_BUFS < GROUPS:
                     load_x(k + LOOKAHEAD + X_BUFS)
+                if k == 0:
+                    keep_warm(WARM_BETWEEN)
                 project(k)
                 for i in range(RUN):
                     copy_values(k, i)

@@ -67,6 +67,7 @@ def tile_multiheadattention_pa_t_kernel(
         trig = ctx.enter_context(tc.tile_pool(name="trig", bufs=2))
         prod_pool = ctx.enter_context(tc.tile_pool(name="products", bufs=2))
         out_pool = ctx.enter_context(tc.tile_pool(name="results", bufs=6))
+        values_pool = ctx.enter_context(tc.tile_pool(name="values", bufs=4))
         xt_pool = ctx.enter_context(tc.psum_pool(name="xt", bufs=4))
         sum_pool = ctx.enter_context(tc.psum_pool(name="sums", bufs=4))
 
@@ -94,11 +95,13 @@ def tile_multiheadattention_pa_t_kernel(
         planes = {}
         sums = {}
         results = {}
+        values = {}
         sizes = {}
         products = {}
 
         def pieces(k):
-            return 2 if k >= GROUPS - 2 else 1
+            spans = {GROUPS - 3: (4,), GROUPS - 2: (2, 2), GROUPS - 1: (2, 1, 1)}.get(k, (RUN,))
+            return [(sum(spans[:j]), span) for j, span in enumerate(spans)]
 
         def batch_and_rows(k):
             first = RUN * (k // BATCH)
@@ -203,10 +206,10 @@ def tile_multiheadattention_pa_t_kernel(
                 )
 
         def project(k):
-            span = RUN // pieces(k)
             results[k] = [
-                out_pool.tile([P, ROTATED_HEADS + 1, span, HEAD], F32, name="results") for piece in range(pieces(k))
+                out_pool.tile([P, ROTATED_HEADS, span, HEAD], F32, name="results") for first, span in pieces(k)
             ]
+            values[k] = values_pool.tile([P, RUN, HEAD], F32, name="values")
             products[k] = prod_pool.tile([P, RUN, 2, ROTATED_HEADS, HEAD], F32, name="products")
             for i in range(RUN):
                 sums[k, i] = sum_pool.tile([P, ROTATED_HEADS + 1, HEAD], F32, name="sums")
@@ -231,29 +234,31 @@ def tile_multiheadattention_pa_t_kernel(
             )
 
         def add(engine, k, piece):
-            span = RUN // pieces(k)
-            tiles = slice(span * piece, span * (piece + 1))
+            first, span = pieces(k)[piece]
+            tiles = slice(first, first + span)
             own = products[k][:, tiles, 0].rearrange("p i h (j m) -> p i h j m", m=2)
             other = products[k][:, tiles, 1].rearrange("p i h (j m) -> p i h j m", m=2)
             engine.tensor_tensor(
-                out=results[k][piece][:, 0:ROTATED_HEADS, :, :].rearrange("p h i (j e) -> p i h j e", e=2),
+                out=results[k][piece][:].rearrange("p h i (j e) -> p i h j e", e=2),
                 in0=own,
                 in1=other[:, :, :, :, ::-1],
                 op=ALU.add,
             )
 
         def copy_values(k, i):
-            piece, local = divmod(i, RUN // pieces(k))
-            nc.scalar.copy(out=results[k][piece][:, ROTATED_HEADS, local, :], in_=sums[k, i][:, ROTATED_HEADS, :])
+            nc.scalar.copy(out=values[k][:, i, :], in_=sums[k, i][:, ROTATED_HEADS, :])
+
+        def store_values(k):
+            b, first, beyond = batch_and_rows(k)
+            nc.sync.dma_start(out=v_rows[b, :, 0, first:beyond, :], in_=values[k][:])
 
         def store(k, piece):
-            b, first, beyond = batch_and_rows(k)
-            span = RUN // pieces(k)
-            r0 = first + span * piece
+            b, r0, beyond = batch_and_rows(k)
+            first, span = pieces(k)[piece]
+            r0 = r0 + first
             r1 = r0 + span
             nc.sync.dma_start(out=q_rows[b, :, :, r0:r1, :], in_=results[k][piece][:, 0:2, :, :])
             nc.sync.dma_start(out=k_rows[b, :, 0, r0:r1, :], in_=results[k][piece][:, 2, :, :])
-            nc.sync.dma_start(out=v_rows[b, :, 0, r0:r1, :], in_=results[k][piece][:, 3, :, :])
 
         with tc.manual_schedule():
             nc.vector.memset(w_planes[:].bitcast(I32), 0)
@@ -319,13 +324,16 @@ def tile_multiheadattention_pa_t_kernel(
                     copy_values(k, i)
                     if i > 0 and k // BATCH + 1 < SLICES:
                         fill_table(k // BATCH + 1, (RUN - 1) * (k % BATCH) + i - 1)
+                store_values(k)
+                if k > 0:
+                    for piece in range(len(pieces(k - 1))):
+                        store(k - 1, piece)
                 for i in range(RUN):
                     multiply(k, i)
                 adder = nc.gpsimd if k < GROUPS - 1 else nc.vector
-                add(adder, k, 0)
-                if k + LOOKAHEAD < GROUPS:
-                    quantise(k + LOOKAHEAD)
-                store(k, 0)
-                for piece in range(1, pieces(k)):
+                for piece in range(len(pieces(k))):
                     add(adder, k, piece)
-                    store(k, piece)
+                    if piece == 0 and k + LOOKAHEAD < GROUPS:
+                        quantise(k + LOOKAHEAD)
+                    if k == GROUPS - 1:
+                        store(k, piece)

@@ -26,13 +26,20 @@ PASSES = D_MODEL // K_PASS
 PASS_WORDS = K_PASS // 2
 ROWS = SEQ // P
 RUN = 4
-SLICES = ROWS // RUN
+SIZES = (2, 2) + 7 * (RUN,)
+STARTS = tuple([sum(SIZES[:c]) for c in range(len(SIZES))])
+SLICES = len(SIZES)
 GROUPS = BATCH * SLICES
 X_BUFS = 6
-TABLE_PARTS = 6
-WARM_FIRST = 7
-WARM_BETWEEN = 2
+WARM = {0: 5, 1: 2, 2: 2, "P0": 2}
+TAIL = {2: (2, 2), 1: (2, 1, 1)}
+VEC_ADDS = 0
+DMA_ORDER = "x0 s0 s1 s2 s3 s4 s5 x1 s6 s7 s8 s9 s10 s11 x2 w0 w1 w2 x3 x4 x5"
+ROWS_AT = {"start": ((0, 2), (2, 4)), "T1": ((4, 10), (10, 16)), "Q1": ((16, 24), (24, 32))}
+FILL_AT = 1
 LOOKAHEAD = 2
+FIRST_LOOKAHEAD = 2
+RAMP = 0
 QUADRANTS = 4
 
 ROPE_BASE = 10000.0
@@ -42,7 +49,7 @@ ROUND_MAGIC = 1.5 * 2.0**23
 FLOPS = 2 * BATCH * SEQ * D_MODEL * N_OUT
 
 assert 4**3 == PAIRS
-assert TABLE_PARTS == BATCH * (RUN - 1)
+assert sum(SIZES) == ROWS
 
 
 def tile_multiheadattention_pa_t_kernel(
@@ -86,7 +93,7 @@ def tile_multiheadattention_pa_t_kernel(
         rounded = const.tile([P, ROWS, PAIRS], F32, name="rounded")
         excess = const.tile([P, 2, ROWS, PAIRS], F32, name="excess")
         table = [
-            const.tile([P, RUN, 2, PAIRS, 2], F32, name="table%d" % c) for c in range(SLICES)
+            const.tile([P, SIZES[c], 2, PAIRS, 2], F32, name="table%d" % c) for c in range(SLICES)
         ]
 
         x_tiles = {}
@@ -100,12 +107,15 @@ def tile_multiheadattention_pa_t_kernel(
         products = {}
 
         def pieces(k):
-            spans = {GROUPS - 3: (4,), GROUPS - 2: (2, 2), GROUPS - 1: (2, 1, 1)}.get(k, (RUN,))
+            spans = TAIL.get(GROUPS - k, (size(k),))
             return [(sum(spans[:j]), span) for j, span in enumerate(spans)]
 
         def batch_and_rows(k):
-            first = RUN * (k // BATCH)
-            return k % BATCH, first, first + RUN
+            first = STARTS[k // BATCH]
+            return k % BATCH, first, first + size(k)
+
+        def size(k):
+            return SIZES[k // BATCH]
 
         def load_scale_rows(scales, first, width, quadrant):
             nc.sync.dma_start(
@@ -115,7 +125,7 @@ def tile_multiheadattention_pa_t_kernel(
 
         def load_x(k):
             b, r0, r1 = batch_and_rows(k)
-            x_tiles[k] = x_pool.tile([P, RUN, D_MODEL], BF16, name="x_tile")
+            x_tiles[k] = x_pool.tile([P, r1 - r0, D_MODEL], BF16, name="x_tile")
             nc.sync.dma_start(out=x_tiles[k][:], in_=x_rows[b, :, r0:r1, :])
 
         def reduce_phase(*chunks):
@@ -141,38 +151,46 @@ def tile_multiheadattention_pa_t_kernel(
                     op1=ALU.subtract,
                 )
 
-        def fill_table(c, part):
-            rows = slice(RUN * c, RUN * (c + 1))
-            if part == 0:
-                sizes[c] = trig.tile([P, RUN, PAIRS], F32, name="size")
+        def table_parts(c):
+            n = SIZES[c]
+            first = STARTS[c]
+            rows = slice(first, first + n)
+            sizes[c] = trig.tile([P, n, PAIRS], F32, name="size")
+
+            def magnitude():
                 nc.scalar.activation(out=sizes[c][:], in_=excess[:, 1, rows, :], func=ACT.Abs)
-            elif part == 1:
+
+            def negative():
                 nc.scalar.activation(out=excess[:, 0, rows, :], in_=excess[:, 1, rows, :], func=ACT.Copy, scale=-1.0)
-            else:
-                a, half = divmod(part - 2, 2)
-                i0 = half * (RUN // 2)
-                i1 = i0 + RUN // 2
-                if a == 0:
-                    nc.scalar.activation(
-                        out=table[c][:, i0:i1, 0, :, :],
-                        in_=sizes[c][:, i0:i1, :].unsqueeze(3).to_broadcast([P, RUN // 2, PAIRS, 2]),
-                        func=ACT.Sin,
-                        scale=-TWO_PI,
-                        bias=0.25 * TWO_PI,
-                    )
-                else:
-                    nc.scalar.activation(
-                        out=table[c][:, i0:i1, 1, :, :],
-                        in_=excess[:, :, RUN * c + i0 : RUN * c + i1, :].rearrange("p m r j -> p r j m"),
-                        func=ACT.Sin,
-                        scale=TWO_PI,
-                    )
+
+            def cosines(i0, i1):
+                nc.scalar.activation(
+                    out=table[c][:, i0:i1, 0, :, :],
+                    in_=sizes[c][:, i0:i1, :].unsqueeze(3).to_broadcast([P, i1 - i0, PAIRS, 2]),
+                    func=ACT.Sin,
+                    scale=-TWO_PI,
+                    bias=0.25 * TWO_PI,
+                )
+
+            def sines(i0, i1):
+                nc.scalar.activation(
+                    out=table[c][:, i0:i1, 1, :, :],
+                    in_=excess[:, :, first + i0 : first + i1, :].rearrange("p m r j -> p r j m"),
+                    func=ACT.Sin,
+                    scale=TWO_PI,
+                )
+
+            parts = [magnitude, negative]
+            for kind in (cosines, sines):
+                for i0 in range(0, n, 2):
+                    parts.append(lambda kind=kind, i0=i0: kind(i0, i0 + 2))
+            return parts
 
         def transpose_group(k):
-            grouped[k] = quant.tile([P, RUN, D_MODEL], BF16, name="grouped", align_bytes=64)
-            codes[k] = code_pool.tile([P, RUN, PASSES * P], U32, name="codes", align_bytes=64)
-            planes[k] = code_pool.tile([P, RUN, PASSES * P], U8, name="planes", align_bytes=64)
-            for i in range(RUN):
+            grouped[k] = quant.tile([P, size(k), D_MODEL], BF16, name="grouped", align_bytes=64)
+            codes[k] = code_pool.tile([P, size(k), PASSES * P], U32, name="codes", align_bytes=64)
+            planes[k] = code_pool.tile([P, size(k), PASSES * P], U8, name="planes", align_bytes=64)
+            for i in range(size(k)):
                 words = x_tiles[k][:, i, :].bitcast(F32)
                 flipped = xt_pool.tile([P, PASSES, 2, P], F32, name="flipped")
                 for g in range(PASSES):
@@ -209,9 +227,9 @@ def tile_multiheadattention_pa_t_kernel(
             results[k] = [
                 out_pool.tile([P, ROTATED_HEADS, span, HEAD], F32, name="results") for first, span in pieces(k)
             ]
-            values[k] = values_pool.tile([P, RUN, HEAD], F32, name="values")
-            products[k] = prod_pool.tile([P, RUN, 2, ROTATED_HEADS, HEAD], F32, name="products")
-            for i in range(RUN):
+            values[k] = values_pool.tile([P, size(k), HEAD], F32, name="values")
+            products[k] = prod_pool.tile([P, size(k), 2, ROTATED_HEADS, HEAD], F32, name="products")
+            for i in range(size(k)):
                 sums[k, i] = sum_pool.tile([P, ROTATED_HEADS + 1, HEAD], F32, name="sums")
                 for g in range(PASSES):
                     nc.tensor.matmul_mx(
@@ -262,7 +280,7 @@ def tile_multiheadattention_pa_t_kernel(
 
         with tc.manual_schedule():
             nc.vector.memset(w_planes[:].bitcast(I32), 0)
-            nc.gpsimd.memset(idle_work[:], 0.0)
+            nc.vector.memset(idle_work[:], 0.0)
             nc.gpsimd.memset(warm[:, 0:1], 0.0)
             nc.scalar.activation(out=warm[:, 1:2], in_=warm[:, 0:1], func=ACT.Sin)
             nc.gpsimd.iota(position_int[:], pattern=[[1, ROWS]], base=0, channel_multiplier=ROWS)
@@ -270,22 +288,21 @@ def tile_multiheadattention_pa_t_kernel(
             scale_loads = [
                 (weight[1], weight[2], weight[3], quadrant) for weight in weights for quadrant in range(QUADRANTS)
             ]
-            load_x(0)
-            for job in scale_loads[0:6]:
-                load_scale_rows(*job)
-            load_x(1)
-            load_scale_rows(*scale_loads[6])
-            for weight in weights:
-                first, width = weight[2], weight[3]
-                nc.scalar.dma_start(
-                    out=w_codes[:, :, first : first + width].bitcast(F32),
-                    in_=weight[0].rearrange("g p n t -> p g (n t)").bitcast(F32),
+            def load_words(j):
+                first, width = weights[j][2], weights[j][3]
+                nc.sync.dma_start(
+                    out=w_codes[:, :, first : first + width].bitcast(I32),
+                    in_=weights[j][0].rearrange("g p n t -> p g (n t)").bitcast(I32),
                 )
-            load_x(2)
-            for job in scale_loads[7:]:
-                load_scale_rows(*job)
-            for k in range(3, X_BUFS):
-                load_x(k)
+
+            for step in DMA_ORDER.split():
+                kind, number = step[0], int(step[1:])
+                if kind == "s":
+                    load_scale_rows(*scale_loads[number])
+                elif kind == "w":
+                    load_words(number)
+                else:
+                    load_x(number)
 
             nc.vector.memset(one[:], 1.0)
             nc.vector.tensor_scalar(out=turns[:, 0:1], in0=one[:], scalar1=1.0 / TWO_PI, scalar2=None, op0=ALU.mult)
@@ -299,41 +316,68 @@ def tile_multiheadattention_pa_t_kernel(
                         op0=ALU.mult,
                     )
             nc.vector.tensor_copy(out=position[:], in_=position_int[:])
-            reduce_phase((0, RUN), (RUN, ROWS // 2))
-            for part in range(TABLE_PARTS):
-                fill_table(0, part)
-            reduce_phase((ROWS // 2, 3 * ROWS // 4), (3 * ROWS // 4, ROWS))
+            def rows_at(event):
+                for j in range(0, len(ROWS_AT.get(event, ())), 2):
+                    reduce_phase(*ROWS_AT[event][j : j + 2])
 
-            keep_warm(WARM_FIRST)
-            for k in range(LOOKAHEAD):
-                transpose_group(k)
-                load_x(k + X_BUFS)
-                keep_warm(WARM_BETWEEN)
-            for k in range(LOOKAHEAD):
-                quantise(k)
+            rows_at("start")
+            state = dict(transposed=0, quantised=0, loaded=X_BUFS)
+            parts = []
+
+            def transpose_up_to(n):
+                while state["transposed"] < min(n, GROUPS):
+                    k = state["transposed"]
+                    if k in WARM:
+                        keep_warm(WARM[k])
+                    transpose_group(k)
+                    if k == FILL_AT:
+                        for part in table_parts(0):
+                            part()
+                    if state["loaded"] < GROUPS:
+                        load_x(state["loaded"])
+                        state["loaded"] += 1
+                    state["transposed"] += 1
+                    rows_at("T%d" % k)
+
+            def quantise_up_to(n):
+                while state["quantised"] < min(n, state["transposed"]):
+                    quantise(state["quantised"])
+                    rows_at("Q%d" % state["quantised"])
+                    state["quantised"] += 1
 
             for k in range(GROUPS):
-                if k + LOOKAHEAD < GROUPS:
-                    transpose_group(k + LOOKAHEAD)
-                if k + LOOKAHEAD + X_BUFS < GROUPS:
-                    load_x(k + LOOKAHEAD + X_BUFS)
+                ahead = FIRST_LOOKAHEAD if k < RAMP else LOOKAHEAD
                 if k == 0:
-                    keep_warm(WARM_BETWEEN)
+                    transpose_up_to(ahead)
+                    quantise_up_to(ahead)
+                transpose_up_to(k + 1 + ahead)
+                quantise_up_to(k + 1)
+                if k == 0 and "P0" in WARM:
+                    keep_warm(WARM["P0"])
                 project(k)
-                for i in range(RUN):
+                if k % BATCH == 0 and k // BATCH + 1 < SLICES:
+                    parts = table_parts(k // BATCH + 1)
+                slots = (size(k) - 1) * (BATCH - k % BATCH)
+                for i in range(size(k)):
                     copy_values(k, i)
-                    if i > 0 and k // BATCH + 1 < SLICES:
-                        fill_table(k // BATCH + 1, (RUN - 1) * (k % BATCH) + i - 1)
+                    if i > 0:
+                        take = -(-len(parts) // slots)
+                        for part in parts[:take]:
+                            part()
+                        parts = parts[take:]
+                        slots -= 1
                 store_values(k)
                 if k > 0:
                     for piece in range(len(pieces(k - 1))):
                         store(k - 1, piece)
-                for i in range(RUN):
+                for i in range(size(k)):
                     multiply(k, i)
-                adder = nc.gpsimd if k < GROUPS - 1 else nc.vector
+                rows_at("M%d" % k)
+                adder = nc.gpsimd if VEC_ADDS <= k < GROUPS - 1 else nc.vector
                 for piece in range(len(pieces(k))):
                     add(adder, k, piece)
-                    if piece == 0 and k + LOOKAHEAD < GROUPS:
-                        quantise(k + LOOKAHEAD)
+                    if piece == 0:
+                        quantise_up_to(GROUPS)
+                        rows_at("A%d" % k)
                     if k == GROUPS - 1:
                         store(k, piece)

@@ -35,7 +35,7 @@ WARM = {0: 5, 1: 2, 2: 2, "P0": 2}
 TAIL = {2: (2, 2), 1: (2, 1, 1)}
 VEC_ADDS = 0
 DMA_ORDER = "x0 s0 s1 s2 s3 s4 s5 x1 s6 s7 s8 s9 s10 s11 x2 w0 w1 w2 x3 x4 x5"
-ROWS_AT = {"start": ((0, 2), (2, 4)), "T1": ((4, 10), (10, 16)), "Q1": ((16, 24), (24, 32))}
+ROWS_AT = {"start": ((0, 4), (4, 16)), "Q1": ((16, 24), (24, 32))}
 FILL_AT = 1
 LOOKAHEAD = 2
 FIRST_LOOKAHEAD = 2
@@ -45,6 +45,8 @@ QUADRANTS = 4
 ROPE_BASE = 10000.0
 TWO_PI = 2.0 * math.pi
 ROUND_MAGIC = 1.5 * 2.0**23
+
+TURNING = sum(1 for j in range(PAIRS) if (SEQ - 1) * ROPE_BASE ** (-j / PAIRS) >= 0.5 * TWO_PI)
 
 FLOPS = 2 * BATCH * SEQ * D_MODEL * N_OUT
 
@@ -74,23 +76,22 @@ def tile_multiheadattention_pa_t_kernel(
         trig = ctx.enter_context(tc.tile_pool(name="trig", bufs=2))
         prod_pool = ctx.enter_context(tc.tile_pool(name="products", bufs=2))
         out_pool = ctx.enter_context(tc.tile_pool(name="results", bufs=6))
-        values_pool = ctx.enter_context(tc.tile_pool(name="values", bufs=4))
+        values_pool = ctx.enter_context(tc.tile_pool(name="values", bufs=6))
         xt_pool = ctx.enter_context(tc.psum_pool(name="xt", bufs=4))
         sum_pool = ctx.enter_context(tc.psum_pool(name="sums", bufs=4))
 
         identity = const.tile([P, P], F32, name="identity")
         make_identity(nc, identity[:])
 
-        w_codes = const.tile([P, PASSES, N_OUT], U32, name="w_codes", align_bytes=64)
-        w_planes = const.tile([P, PASSES, N_OUT], U8, name="w_planes", align_bytes=64)
+        w_codes = const.tile([P, PASSES, N_OUT], U32, name="w_codes", align_bytes=256)
+        w_planes = const.tile([P, PASSES, N_OUT], U8, name="w_planes", align_bytes=256)
         position_int = const.tile([P, ROWS], I32, name="position_int")
         position = const.tile([P, ROWS], F32, name="position")
         one = const.tile([P, 1], F32, name="one")
         idle_work = const.tile([P, N_OUT], BF16, name="idle_work")
         warm = const.tile([P, 2], F32, name="warm")
         turns = const.tile([P, PAIRS], F32, name="turns")
-        phase = const.tile([P, ROWS, PAIRS], F32, name="phase")
-        rounded = const.tile([P, ROWS, PAIRS], F32, name="rounded")
+        rounded = const.tile([P, ROWS, TURNING], F32, name="rounded")
         excess = const.tile([P, 2, ROWS, PAIRS], F32, name="excess")
         table = [
             const.tile([P, SIZES[c], 2, PAIRS, 2], F32, name="table%d" % c) for c in range(SLICES)
@@ -132,21 +133,25 @@ def tile_multiheadattention_pa_t_kernel(
             for r0, r1 in chunks:
                 shape = [P, r1 - r0, PAIRS]
                 nc.vector.tensor_tensor(
-                    out=phase[:, r0:r1, :],
+                    out=excess[:, 1, r0:r1, :],
                     in0=position[:, r0:r1].unsqueeze(2).to_broadcast(shape),
                     in1=turns[:].unsqueeze(1).to_broadcast(shape),
                     op=ALU.mult,
                 )
             for r0, r1 in chunks:
                 nc.vector.tensor_scalar(
-                    out=rounded[:, r0:r1, :], in0=phase[:, r0:r1, :], scalar1=ROUND_MAGIC, scalar2=None, op0=ALU.add
+                    out=rounded[:, r0:r1, :],
+                    in0=excess[:, 1, r0:r1, 0:TURNING],
+                    scalar1=ROUND_MAGIC,
+                    scalar2=None,
+                    op0=ALU.add,
                 )
             for r0, r1 in chunks:
                 nc.vector.scalar_tensor_tensor(
-                    out=excess[:, 1, r0:r1, :],
+                    out=excess[:, 1, r0:r1, 0:TURNING],
                     in0=rounded[:, r0:r1, :],
                     scalar=ROUND_MAGIC,
-                    in1=phase[:, r0:r1, :],
+                    in1=excess[:, 1, r0:r1, 0:TURNING],
                     op0=ALU.subtract,
                     op1=ALU.subtract,
                 )
@@ -187,9 +192,9 @@ def tile_multiheadattention_pa_t_kernel(
             return parts
 
         def transpose_group(k):
-            grouped[k] = quant.tile([P, size(k), D_MODEL], BF16, name="grouped", align_bytes=64)
-            codes[k] = code_pool.tile([P, size(k), PASSES * P], U32, name="codes", align_bytes=64)
-            planes[k] = code_pool.tile([P, size(k), PASSES * P], U8, name="planes", align_bytes=64)
+            grouped[k] = quant.tile([P, size(k), D_MODEL], BF16, name="grouped", align_bytes=256)
+            codes[k] = code_pool.tile([P, size(k), PASSES * P], U32, name="codes", align_bytes=256)
+            planes[k] = code_pool.tile([P, size(k), PASSES * P], U8, name="planes", align_bytes=256)
             for i in range(size(k)):
                 words = x_tiles[k][:, i, :].bitcast(F32)
                 flipped = xt_pool.tile([P, PASSES, 2, P], F32, name="flipped")
@@ -315,6 +320,9 @@ def tile_multiheadattention_pa_t_kernel(
                         scalar2=None,
                         op0=ALU.mult,
                     )
+            nc.vector.tensor_scalar(
+                out=turns[:, TURNING:], in0=turns[:, TURNING:], scalar1=-1.0, scalar2=None, op0=ALU.mult
+            )
             nc.vector.tensor_copy(out=position[:], in_=position_int[:])
             def rows_at(event):
                 for j in range(0, len(ROWS_AT.get(event, ())), 2):

@@ -37,6 +37,7 @@ VEC_ADDS = 0
 DMA_ORDER = "x0 s0 s1 s2 s3 s4 s5 x1 s6 s7 s8 s9 s10 s11 x2 w0 w1 w2 x3 x4 x5"
 ROWS_AT = {"start": ((0, 4), (4, 16)), "Q1": ((16, 24), (24, 32))}
 FILL_AT = 1
+SPLIT_FROM = 4
 LOOKAHEAD = 2
 FIRST_LOOKAHEAD = 2
 RAMP = 0
@@ -191,11 +192,13 @@ def tile_multiheadattention_pa_t_kernel(
                     parts.append(lambda kind=kind, i0=i0: kind(i0, i0 + 2))
             return parts
 
-        def transpose_group(k):
-            grouped[k] = quant.tile([P, size(k), D_MODEL], BF16, name="grouped", align_bytes=256)
-            codes[k] = code_pool.tile([P, size(k), PASSES * P], U32, name="codes", align_bytes=256)
-            planes[k] = code_pool.tile([P, size(k), PASSES * P], U8, name="planes", align_bytes=256)
-            for i in range(size(k)):
+        def transpose_group(k, tiles=None):
+            tiles = range(size(k)) if tiles is None else tiles
+            if 0 in tiles:
+                grouped[k] = quant.tile([P, size(k), D_MODEL], BF16, name="grouped", align_bytes=256)
+                codes[k] = code_pool.tile([P, size(k), PASSES * P], U32, name="codes", align_bytes=256)
+                planes[k] = code_pool.tile([P, size(k), PASSES * P], U8, name="planes", align_bytes=256)
+            for i in tiles:
                 words = x_tiles[k][:, i, :].bitcast(F32)
                 flipped = xt_pool.tile([P, PASSES, 2, P], F32, name="flipped")
                 for g in range(PASSES):
@@ -228,13 +231,10 @@ def tile_multiheadattention_pa_t_kernel(
                     stop=True,
                 )
 
-        def project(k):
-            results[k] = [
-                out_pool.tile([P, ROTATED_HEADS, span, HEAD], F32, name="results") for first, span in pieces(k)
-            ]
-            values[k] = values_pool.tile([P, size(k), HEAD], F32, name="values")
-            products[k] = prod_pool.tile([P, size(k), 2, ROTATED_HEADS, HEAD], F32, name="products")
-            for i in range(size(k)):
+        def project(k, tiles):
+            if 0 in tiles:
+                start_group(k)
+            for i in tiles:
                 sums[k, i] = sum_pool.tile([P, ROTATED_HEADS + 1, HEAD], F32, name="sums")
                 for g in range(PASSES):
                     nc.tensor.matmul_mx(
@@ -246,6 +246,13 @@ def tile_multiheadattention_pa_t_kernel(
                         start=(g == 0),
                         stop=(g == PASSES - 1),
                     )
+
+        def start_group(k):
+            results[k] = [
+                out_pool.tile([P, ROTATED_HEADS, span, HEAD], F32, name="results") for first, span in pieces(k)
+            ]
+            values[k] = values_pool.tile([P, size(k), HEAD], F32, name="values")
+            products[k] = prod_pool.tile([P, size(k), 2, ROTATED_HEADS, HEAD], F32, name="products")
 
         def multiply(k, i):
             shape = [P, 2, ROTATED_HEADS, HEAD]
@@ -358,15 +365,27 @@ def tile_multiheadattention_pa_t_kernel(
                 if k == 0:
                     transpose_up_to(ahead)
                     quantise_up_to(ahead)
-                transpose_up_to(k + 1 + ahead)
+                ahead_k = k + ahead
+                split = ahead_k < GROUPS and size(k) == RUN and size(ahead_k) == RUN and k >= SPLIT_FROM
+                if not split:
+                    transpose_up_to(k + 1 + ahead)
                 quantise_up_to(k + 1)
                 if k == 0 and "P0" in WARM:
                     keep_warm(WARM["P0"])
-                project(k)
                 if k % BATCH == 0 and k // BATCH + 1 < SLICES:
                     parts = table_parts(k // BATCH + 1)
                 slots = (size(k) - 1) * (BATCH - k % BATCH)
                 for i in range(size(k)):
+                    half = (i, i + 1) if split else tuple(range(size(k)))
+                    if i == 0 or (split and i == 2):
+                        if split:
+                            transpose_group(ahead_k, half)
+                            if i == 2:
+                                state["transposed"] += 1
+                                if state["loaded"] < GROUPS:
+                                    load_x(state["loaded"])
+                                    state["loaded"] += 1
+                        project(k, half)
                     copy_values(k, i)
                     if i > 0:
                         take = -(-len(parts) // slots)

@@ -252,7 +252,12 @@ def tile_multiheadattention_pa_t_kernel(
                 out_pool.tile([P, ROTATED_HEADS, span, HEAD], F32, name="results") for first, span in pieces(k)
             ]
             values[k] = values_pool.tile([P, size(k), HEAD], F32, name="values")
-            products[k] = prod_pool.tile([P, size(k), 2, ROTATED_HEADS, HEAD], F32, name="products")
+            if len(pieces(k)) == 1:
+                whole = prod_pool.tile([P, 2, ROTATED_HEADS, size(k), HEAD], F32, name="products")
+                products[k] = whole[:].rearrange("p a h i d -> p i a h d")
+            else:
+                by_tile = prod_pool.tile([P, size(k), 2, ROTATED_HEADS, HEAD], F32, name="products")
+                products[k] = by_tile[:]
 
         def multiply(k, i):
             shape = [P, 2, ROTATED_HEADS, HEAD]
@@ -266,10 +271,11 @@ def tile_multiheadattention_pa_t_kernel(
         def add(engine, k, piece):
             first, span = pieces(k)[piece]
             tiles = slice(first, first + span)
-            own = products[k][:, tiles, 0].rearrange("p i h (j m) -> p i h j m", m=2)
-            other = products[k][:, tiles, 1].rearrange("p i h (j m) -> p i h j m", m=2)
+            order = "p h i j m" if len(pieces(k)) == 1 else "p i h j m"
+            own = products[k][:, tiles, 0].rearrange("p i h (j m) -> " + order, m=2)
+            other = products[k][:, tiles, 1].rearrange("p i h (j m) -> " + order, m=2)
             engine.tensor_tensor(
-                out=results[k][piece][:].rearrange("p h i (j e) -> p i h j e", e=2),
+                out=results[k][piece][:].rearrange("p h i (j m) -> " + order, m=2),
                 in0=own,
                 in1=other[:, :, :, :, ::-1],
                 op=ALU.add,

import math
from contextlib import ExitStack

import concourse.mybir as mybir
from concourse.masks import make_identity

F32 = mybir.dt.float32
BF16 = mybir.dt.bfloat16
I32 = mybir.dt.int32
U32 = mybir.dt.uint32
U8 = mybir.dt.uint8
FP8X4 = mybir.dt.float8_e4m3fn_x4
ALU = mybir.AluOpType
ACT = mybir.ActivationFunctionType

P = 128
BATCH = 2
SEQ = 4096
D_MODEL = 1024
HEAD = 128
PAIRS = HEAD // 2
ROTATED_HEADS = 3
N_OUT = 4 * HEAD
K_PASS = 4 * P
PASSES = D_MODEL // K_PASS
PASS_WORDS = K_PASS // 2
ROWS = SEQ // P
RUN = 4
SIZES = (2, 2) + 7 * (RUN,)
STARTS = tuple([sum(SIZES[:c]) for c in range(len(SIZES))])
SLICES = len(SIZES)
GROUPS = BATCH * SLICES
X_BUFS = 6
WARM = {0: 5, 1: 2, 2: 2, "P0": 2}
TAIL = {2: (2, 2), 1: (2, 1, 1)}
VEC_ADDS = 0
DMA_ORDER = "x0 s0 s1 s2 s3 s4 s5 x1 s6 s7 s8 s9 s10 s11 x2 w0 w1 w2 x3 x4 x5"
ROWS_AT = {"start": ((0, 4), (4, 16)), "Q1": ((16, 24), (24, 32))}
FILL_AT = 1
SPLIT_FROM = 4
LOOKAHEAD = 2
FIRST_LOOKAHEAD = 2
RAMP = 0
QUADRANTS = 4

ROPE_BASE = 10000.0
TWO_PI = 2.0 * math.pi
ROUND_MAGIC = 1.5 * 2.0**23

TURNING = sum(1 for j in range(PAIRS) if (SEQ - 1) * ROPE_BASE ** (-j / PAIRS) >= 0.5 * TWO_PI)

FLOPS = 2 * BATCH * SEQ * D_MODEL * N_OUT

assert 4**3 == PAIRS
assert sum(SIZES) == ROWS


def tile_multiheadattention_pa_t_kernel(
    tc, x, wq_words, wq_scales, wk_words, wk_scales, wv_words, wv_scales, out_q, out_k, out_v
):
    nc = tc.nc
    weights = (
        (wq_words, wq_scales, 0, 2 * HEAD),
        (wk_words, wk_scales, 2 * HEAD, HEAD),
        (wv_words, wv_scales, 3 * HEAD, HEAD),
    )
    x_rows = x.rearrange("b (p r) k -> b p r k", r=ROWS)
    q_rows = out_q.rearrange("b h (p r) d -> b p h r d", r=ROWS)
    k_rows = out_k.rearrange("b h (p r) d -> b p h r d", r=ROWS)
    v_rows = out_v.rearrange("b h (p r) d -> b p h r d", r=ROWS)

    with ExitStack() as ctx:
        const = ctx.enter_context(tc.tile_pool(name="const", bufs=1))
        x_pool = ctx.enter_context(tc.tile_pool(name="x", bufs=X_BUFS))
        quant = ctx.enter_context(tc.tile_pool(name="quant", bufs=2))
        code_pool = ctx.enter_context(tc.tile_pool(name="codes", bufs=LOOKAHEAD + 1))
        trig = ctx.enter_context(tc.tile_pool(name="trig", bufs=2))
        prod_pool = ctx.enter_context(tc.tile_pool(name="products", bufs=2))
        out_pool = ctx.enter_context(tc.tile_pool(name="results", bufs=6))
        values_pool = ctx.enter_context(tc.tile_pool(name="values", bufs=6))
        xt_pool = ctx.enter_context(tc.psum_pool(name="xt", bufs=4))
        sum_pool = ctx.enter_context(tc.psum_pool(name="sums", bufs=4))

        identity = const.tile([P, P], F32, name="identity")
        make_identity(nc, identity[:])

        w_codes = const.tile([P, PASSES, N_OUT], U32, name="w_codes", align_bytes=256)
        w_planes = const.tile([P, PASSES, N_OUT], U8, name="w_planes", align_bytes=256)
        position_int = const.tile([P, ROWS], I32, name="position_int")
        position = const.tile([P, ROWS], F32, name="position")
        one = const.tile([P, 1], F32, name="one")
        idle_work = const.tile([P, N_OUT], BF16, name="idle_work")
        warm = const.tile([P, 2], F32, name="warm")
        turns = const.tile([P, PAIRS], F32, name="turns")
        rounded = const.tile([P, ROWS, TURNING], F32, name="rounded")
        excess = const.tile([P, 2, ROWS, PAIRS], F32, name="excess")
        table = [
            const.tile([P, SIZES[c], 2, PAIRS, 2], F32, name="table%d" % c) for c in range(SLICES)
        ]

        x_tiles = {}
        grouped = {}
        codes = {}
        planes = {}
        sums = {}
        results = {}
        values = {}
        sizes = {}
        products = {}

        def pieces(k):
            spans = TAIL.get(GROUPS - k, (size(k),))
            return [(sum(spans[:j]), span) for j, span in enumerate(spans)]

        def batch_and_rows(k):
            first = STARTS[k // BATCH]
            return k % BATCH, first, first + size(k)

        def size(k):
            return SIZES[k // BATCH]

        def load_scale_rows(scales, first, width, quadrant):
            nc.sync.dma_start(
                out=w_planes[32 * quadrant : 32 * quadrant + 4, :, first : first + width].bitcast(I32),
                in_=scales[:, 4 * quadrant : 4 * quadrant + 4, :].rearrange("g r n -> r g n").bitcast(I32),
            )

        def load_x(k):
            b, r0, r1 = batch_and_rows(k)
            x_tiles[k] = x_pool.tile([P, r1 - r0, D_MODEL], BF16, name="x_tile")
            nc.sync.dma_start(out=x_tiles[k][:], in_=x_rows[b, :, r0:r1, :])

        def reduce_phase(*chunks):
            for r0, r1 in chunks:
                shape = [P, r1 - r0, PAIRS]
                nc.vector.tensor_tensor(
                    out=excess[:, 1, r0:r1, :],
                    in0=position[:, r0:r1].unsqueeze(2).to_broadcast(shape),
                    in1=turns[:].unsqueeze(1).to_broadcast(shape),
                    op=ALU.mult,
                )
            for r0, r1 in chunks:
                nc.vector.tensor_scalar(
                    out=rounded[:, r0:r1, :],
                    in0=excess[:, 1, r0:r1, 0:TURNING],
                    scalar1=ROUND_MAGIC,
                    scalar2=None,
                    op0=ALU.add,
                )
            for r0, r1 in chunks:
                nc.vector.scalar_tensor_tensor(
                    out=excess[:, 1, r0:r1, 0:TURNING],
                    in0=rounded[:, r0:r1, :],
                    scalar=ROUND_MAGIC,
                    in1=excess[:, 1, r0:r1, 0:TURNING],
                    op0=ALU.subtract,
                    op1=ALU.subtract,
                )

        def table_parts(c):
            n = SIZES[c]
            first = STARTS[c]
            rows = slice(first, first + n)
            sizes[c] = trig.tile([P, n, PAIRS], F32, name="size")

            def magnitude():
                nc.scalar.activation(out=sizes[c][:], in_=excess[:, 1, rows, :], func=ACT.Abs)

            def negative():
                nc.scalar.activation(out=excess[:, 0, rows, :], in_=excess[:, 1, rows, :], func=ACT.Copy, scale=-1.0)

            def cosines(i0, i1):
                nc.scalar.activation(
                    out=table[c][:, i0:i1, 0, :, :],
                    in_=sizes[c][:, i0:i1, :].unsqueeze(3).to_broadcast([P, i1 - i0, PAIRS, 2]),
                    func=ACT.Sin,
                    scale=-TWO_PI,
                    bias=0.25 * TWO_PI,
                )

            def sines(i0, i1):
                nc.scalar.activation(
                    out=table[c][:, i0:i1, 1, :, :],
                    in_=excess[:, :, first + i0 : first + i1, :].rearrange("p m r j -> p r j m"),
                    func=ACT.Sin,
                    scale=TWO_PI,
                )

            parts = [magnitude, negative]
            for kind in (cosines, sines):
                for i0 in range(0, n, 2):
                    parts.append(lambda kind=kind, i0=i0: kind(i0, i0 + 2))
            return parts

        def transpose_group(k, tiles=None):
            tiles = range(size(k)) if tiles is None else tiles
            if 0 in tiles:
                grouped[k] = quant.tile([P, size(k), D_MODEL], BF16, name="grouped", align_bytes=256)
                codes[k] = code_pool.tile([P, size(k), PASSES * P], U32, name="codes", align_bytes=256)
                planes[k] = code_pool.tile([P, size(k), PASSES * P], U8, name="planes", align_bytes=256)
            for i in tiles:
                words = x_tiles[k][:, i, :].bitcast(F32)
                flipped = xt_pool.tile([P, PASSES, 2, P], F32, name="flipped")
                for g in range(PASSES):
                    for u in range(2):
                        nc.tensor.transpose(
                            flipped[:, g, u, :],
                            words[:, PASS_WORDS * g + u : PASS_WORDS * (g + 1) : 2],
                            identity[:],
                        )
                nc.scalar.copy(
                    out=grouped[k][:, i, :].bitcast(F32).rearrange("q (g n u) -> q g n u", g=PASSES, u=2),
                    in_=flipped[:].rearrange("q g u n -> q g n u"),
                )

        def quantise(k):
            nc.vector.quantize_mx(
                out=codes[k][:].rearrange("q i n -> q (i n)").bitcast(FP8X4),
                scales=planes[k][:].rearrange("q i n -> q (i n)"),
                in_=grouped[k][:].rearrange("q i n -> q (i n)"),
            )

        def keep_warm(count):
            unread = sum_pool.tile([P, ROTATED_HEADS + 1, HEAD], F32, name="sums")
            for n in range(count):
                nc.tensor.matmul(
                    out=unread[:].rearrange("p h d -> p (h d)"),
                    lhsT=idle_work[:, 0:P],
                    rhs=idle_work[:],
                    start=True,
                    stop=True,
                )

        def project(k, tiles):
            if 0 in tiles:
                start_group(k)
            for i in tiles:
                sums[k, i] = sum_pool.tile([P, ROTATED_HEADS + 1, HEAD], F32, name="sums")
                for g in range(PASSES):
                    nc.tensor.matmul_mx(
                        out=sums[k, i][:].rearrange("p h d -> p (h d)"),
                        lhsT=codes[k][:, i, P * g : P * (g + 1)].bitcast(FP8X4),
                        lhsT_scale=planes[k][:, i, P * g : P * (g + 1)],
                        rhs=w_codes[:, g, :].bitcast(FP8X4),
                        rhs_scale=w_planes[:, g, :],
                        start=(g == 0),
                        stop=(g == PASSES - 1),
                    )

        def start_group(k):
            results[k] = [
                out_pool.tile([P, ROTATED_HEADS, span, HEAD], F32, name="results") for first, span in pieces(k)
            ]
            values[k] = values_pool.tile([P, size(k), HEAD], F32, name="values")
            if len(pieces(k)) == 1:
                whole = prod_pool.tile([P, 2, ROTATED_HEADS, size(k), HEAD], F32, name="products")
                products[k] = whole[:].rearrange("p a h i d -> p i a h d")
            else:
                by_tile = prod_pool.tile([P, size(k), 2, ROTATED_HEADS, HEAD], F32, name="products")
                products[k] = by_tile[:]

        def multiply(k, i):
            shape = [P, 2, ROTATED_HEADS, HEAD]
            nc.vector.tensor_tensor(
                out=products[k][:, i],
                in0=sums[k, i][:, 0:ROTATED_HEADS, :].unsqueeze(1).to_broadcast(shape),
                in1=table[k // BATCH][:, i].rearrange("p a j m -> p a (j m)").unsqueeze(2).to_broadcast(shape),
                op=ALU.mult,
            )

        def add(engine, k, piece):
            first, span = pieces(k)[piece]
            tiles = slice(first, first + span)
            order = "p h i j m" if len(pieces(k)) == 1 else "p i h j m"
            own = products[k][:, tiles, 0].rearrange("p i h (j m) -> " + order, m=2)
            other = products[k][:, tiles, 1].rearrange("p i h (j m) -> " + order, m=2)
            engine.tensor_tensor(
                out=results[k][piece][:].rearrange("p h i (j m) -> " + order, m=2),
                in0=own,
                in1=other[:, :, :, :, ::-1],
                op=ALU.add,
            )

        def copy_values(k, i):
            nc.scalar.copy(out=values[k][:, i, :], in_=sums[k, i][:, ROTATED_HEADS, :])

        def store_values(k):
            b, first, beyond = batch_and_rows(k)
            nc.sync.dma_start(out=v_rows[b, :, 0, first:beyond, :], in_=values[k][:])

        def store(k, piece):
            b, r0, beyond = batch_and_rows(k)
            first, span = pieces(k)[piece]
            r0 = r0 + first
            r1 = r0 + span
            nc.sync.dma_start(out=q_rows[b, :, :, r0:r1, :], in_=results[k][piece][:, 0:2, :, :])
            nc.sync.dma_start(out=k_rows[b, :, 0, r0:r1, :], in_=results[k][piece][:, 2, :, :])

        with tc.manual_schedule():
            nc.vector.memset(w_planes[:].bitcast(I32), 0)
            nc.vector.memset(idle_work[:], 0.0)
            nc.gpsimd.memset(warm[:, 0:1], 0.0)
            nc.scalar.activation(out=warm[:, 1:2], in_=warm[:, 0:1], func=ACT.Sin)
            nc.gpsimd.iota(position_int[:], pattern=[[1, ROWS]], base=0, channel_multiplier=ROWS)

            scale_loads = [
                (weight[1], weight[2], weight[3], quadrant) for weight in weights for quadrant in range(QUADRANTS)
            ]
            def load_words(j):
                first, width = weights[j][2], weights[j][3]
                nc.sync.dma_start(
                    out=w_codes[:, :, first : first + width].bitcast(I32),
                    in_=weights[j][0].rearrange("g p n t -> p g (n t)").bitcast(I32),
                )

            for step in DMA_ORDER.split():
                kind, number = step[0], int(step[1:])
                if kind == "s":
                    load_scale_rows(*scale_loads[number])
                elif kind == "w":
                    load_words(number)
                else:
                    load_x(number)

            nc.vector.memset(one[:], 1.0)
            nc.vector.tensor_scalar(out=turns[:, 0:1], in0=one[:], scalar1=1.0 / TWO_PI, scalar2=None, op0=ALU.mult)
            for have in (1, 4, 16):
                for m in range(1, 4):
                    nc.vector.tensor_scalar(
                        out=turns[:, m * have : (m + 1) * have],
                        in0=turns[:, 0:have],
                        scalar1=ROPE_BASE ** (-m * have / PAIRS),
                        scalar2=None,
                        op0=ALU.mult,
                    )
            nc.vector.tensor_scalar(
                out=turns[:, TURNING:], in0=turns[:, TURNING:], scalar1=-1.0, scalar2=None, op0=ALU.mult
            )
            nc.vector.tensor_copy(out=position[:], in_=position_int[:])
            def rows_at(event):
                for j in range(0, len(ROWS_AT.get(event, ())), 2):
                    reduce_phase(*ROWS_AT[event][j : j + 2])

            rows_at("start")
            state = dict(transposed=0, quantised=0, loaded=X_BUFS)
            parts = []

            def transpose_up_to(n):
                while state["transposed"] < min(n, GROUPS):
                    k = state["transposed"]
                    if k in WARM:
                        keep_warm(WARM[k])
                    transpose_group(k)
                    if k == FILL_AT:
                        for part in table_parts(0):
                            part()
                    if state["loaded"] < GROUPS:
                        load_x(state["loaded"])
                        state["loaded"] += 1
                    state["transposed"] += 1
                    rows_at("T%d" % k)

            def quantise_up_to(n):
                while state["quantised"] < min(n, state["transposed"]):
                    quantise(state["quantised"])
                    rows_at("Q%d" % state["quantised"])
                    state["quantised"] += 1

            for k in range(GROUPS):
                ahead = FIRST_LOOKAHEAD if k < RAMP else LOOKAHEAD
                if k == 0:
                    transpose_up_to(ahead)
                    quantise_up_to(ahead)
                ahead_k = k + ahead
                split = ahead_k < GROUPS and size(k) == RUN and size(ahead_k) == RUN and k >= SPLIT_FROM
                if not split:
                    transpose_up_to(k + 1 + ahead)
                quantise_up_to(k + 1)
                if k == 0 and "P0" in WARM:
                    keep_warm(WARM["P0"])
                if k % BATCH == 0 and k // BATCH + 1 < SLICES:
                    parts = table_parts(k // BATCH + 1)
                slots = (size(k) - 1) * (BATCH - k % BATCH)
                for i in range(size(k)):
                    half = (i, i + 1) if split else tuple(range(size(k)))
                    if i == 0 or (split and i == 2):
                        if split:
                            transpose_group(ahead_k, half)
                            if i == 2:
                                state["transposed"] += 1
                                if state["loaded"] < GROUPS:
                                    load_x(state["loaded"])
                                    state["loaded"] += 1
                        project(k, half)
                    copy_values(k, i)
                    if i > 0:
                        take = -(-len(parts) // slots)
                        for part in parts[:take]:
                            part()
                        parts = parts[take:]
                        slots -= 1
                store_values(k)
                if k > 0:
                    for piece in range(len(pieces(k - 1))):
                        store(k - 1, piece)
                for i in range(size(k)):
                    multiply(k, i)
                rows_at("M%d" % k)
                adder = nc.gpsimd if VEC_ADDS <= k < GROUPS - 1 else nc.vector
                for piece in range(len(pieces(k))):
                    add(adder, k, piece)
                    if piece == 0:
                        quantise_up_to(GROUPS)
                        rows_at("A%d" % k)
                    if k == GROUPS - 1:
                        store(k, piece)
